import numpy as np
import ml_dtypes


def mxq(x, axis, fmt="e4m3"):
    dtype, down = {"e4m3": (ml_dtypes.float8_e4m3fn, 7), "e5m2": (ml_dtypes.float8_e5m2, 14)}[fmt]
    v = np.moveaxis(np.asarray(x, np.float32).astype(ml_dtypes.bfloat16).astype(np.float64), axis, -1)
    blocks = v.reshape(v.shape[:-1] + (-1, 32))
    amax = np.abs(blocks).max(-1, keepdims=True)
    byte = np.maximum(np.where(amax > 0, np.frexp(amax)[1] - 1 + 127, 0) - down, 1)
    scale = np.exp2(byte - 127.0)
    codes = (blocks / scale).astype(np.float32).astype(dtype).astype(np.float64)
    return np.moveaxis((codes * scale).reshape(v.shape), -1, axis)


WIDE = False


def mx_kscale(k):
    if not WIDE:
        return np.ones(k)
    levels = np.array([10, -10, 5, -5, 0])
    a = np.random.permutation(np.resize(levels, k // 512 * 4)).reshape(k // 512, 4)
    idx = np.arange(k)
    return np.exp2(a[idx // 512, idx % 128 // 32])


BF16 = ml_dtypes.bfloat16


def bf(x):
    return np.asarray(x, np.float32).astype(BF16)


def f64(x):
    return np.asarray(x).astype(np.float64)


E2M1 = np.array([0.0, 0.5, 1.0, 1.5, 2.0, 3.0, 4.0, 6.0, -0.0, -0.5, -1.0, -1.5, -2.0, -3.0, -4.0, -6.0])


def pack_weight(w, fmt):
    k, n = w.shape
    w = f64(bf(w)).reshape(k // 32, 32, n)
    amax = np.abs(w).max(1)
    if fmt == "e4m3":
        byte = np.frexp(amax)[1] - 1 + 127 - 7
    else:
        mant, ex = np.frexp(amax / 6.0)
        byte = np.where(mant > 0.5, ex, ex - 1) + 127
    byte = np.clip(np.where(amax > 0, byte, 1), 1, 254)
    scaled = (w * np.exp2(127.0 - byte)[:, None, :]).reshape(k, n).astype(np.float32)
    by_word = np.ascontiguousarray(scaled.reshape(k // 512, 128, 4, n).transpose(0, 1, 3, 2))
    if fmt == "e4m3":
        words = by_word.astype(ml_dtypes.float8_e4m3fn).view(np.uint8)
    else:
        c = by_word.astype(ml_dtypes.float4_e2m1fn).view(np.uint8) & 0xF
        words = c[..., 0::2] | (c[..., 1::2] << 4)
    return np.ascontiguousarray(words), np.ascontiguousarray(byte.astype(np.uint8).reshape(k // 512, 16, n))


def unpack_weight(words, scales, fmt):
    g, p, n, _ = words.shape
    if fmt == "e4m3":
        vals = np.ascontiguousarray(words).view(ml_dtypes.float8_e4m3fn).astype(np.float64)
    else:
        nib = np.empty((g, p, n, 4), np.uint8)
        nib[..., 0::2] = words & 0xF
        nib[..., 1::2] = words >> 4
        vals = E2M1[nib]
    vals = vals * np.repeat(np.exp2(scales.astype(np.float64) - 127.0), 8, axis=1)[..., None]
    return vals.transpose(0, 1, 3, 2).reshape(g * 512, n)

def pack4(w):
    words, scales = pack_weight(w, "e2m1")
    return words.reshape(words.shape[0], 128, -1), scales


def unpack4(words, scales):
    return unpack_weight(words.reshape(words.shape[0], 128, -1, 2), scales, "e2m1")


B, DI, DH = 256, 16384, 128


def sigmoid(v):
    return 1.0 / (1.0 + np.exp(-v))


def setup_inputs():
    s = mx_kscale(DI)
    n = np.random.standard_normal
    a, c = 0.7 / np.sqrt(DI), 0.7 / np.sqrt(DH)
    keep = np.random.uniform(size=B) < 0.9
    out = {
        "x": bf(n((B, DI)) * s),
        "h_minors": bf(n((B, DH))),
        "c_minors": bf(n((B, DH))),
        "s0": bf(n((B, DH))),
        "s1": bf(n((B, DH))),
        "s2": bf(n((B, DH))),
        "mask": bf(keep * (0.5 + 0.5 * np.random.uniform(size=B))),
    }
    words, scales = pack4((n((7 * DH, DI)) * a / s).T)
    out["weight_ih_words"] = words
    out["weight_ih_scales"] = scales
    out.update({
        "bias_ih": bf(n(7 * DH) * 0.3),
        "weight_hh": bf(n((4 * DH, DH)) * c),
        "bias_hh": bf(n(4 * DH) * 0.3),
        "weight_sh0": bf(n((DH, DH)) * c),
        "bias_sh0": bf(n(DH) * 0.3),
        "weight_sh1": bf(n((DH, DH)) * c),
        "bias_sh1": bf(n(DH) * 0.3),
        "weight_sh2": bf(n((DH, DH)) * c),
        "bias_sh2": bf(n(DH) * 0.3),
    })
    return out


def reference(x, h_minors, c_minors, s0, s1, s2, mask, weight_ih_words, weight_ih_scales, bias_ih, weight_hh, bias_hh,
              weight_sh0, bias_sh0, weight_sh1, bias_sh1, weight_sh2, bias_sh2):
    d = DH
    m = f64(mask)[:, None]

    tmp = (mxq(f64(x), 1, "e4m3") @ unpack4(weight_ih_words, weight_ih_scales)) + f64(bias_ih)
    tmp2 = f64(h_minors) @ f64(weight_hh).T + f64(bias_hh)
    tmp3 = np.concatenate([
        f64(s0) @ f64(weight_sh0).T + f64(bias_sh0),
        f64(s1) @ f64(weight_sh1).T + f64(bias_sh1),
        f64(s2) @ f64(weight_sh2).T + f64(bias_sh2),
    ], axis=1)

    tmp_in, tmp_s = tmp[:, :4 * d], tmp[:, 4 * d:]
    pre = tmp_in + tmp2
    ifo = sigmoid(pre[:, :3 * d])
    c_hat = pre[:, 3 * d:]
    i_g, f_g, o_g = ifo[:, :d], ifo[:, d:2 * d], ifo[:, 2 * d:]

    c_t = (f_g * f64(c_minors) + i_g * np.tanh(c_hat)) * m
    tc = np.tanh(c_t) * m
    h = o_g * tc

    bg = sigmoid(tmp_s + tmp3)
    b0, b1, b2 = bg[:, :d], bg[:, d:2 * d], bg[:, 2 * d:]

    s_0 = (b0 + 1.0 - o_g) * tc
    s_1 = (b1 + 2.0 - o_g - s_0) * 0.5 * tc
    s_2 = (b2 + 3.0 - o_g - (2.0 * s_0 + s_1)) * (1.0 / 3.0) * tc

    return (h, c_t, s_0, s_1, s_2)

@@ -1,0 +1,337 @@
+from contextlib import ExitStack
+
+import concourse.mybir as mybir
+from concourse.masks import make_identity
+
+F32 = mybir.dt.float32
+BF16 = mybir.dt.bfloat16
+I32 = mybir.dt.int32
+U32 = mybir.dt.uint32
+U8 = mybir.dt.uint8
+FP8X4 = mybir.dt.float8_e4m3fn_x4
+FP4X4 = mybir.dt.float4_e2m1fn_x4
+ACT = mybir.ActivationFunctionType
+ALU = mybir.AluOpType
+
+P = 128
+BATCH, D_IN, D_H = 256, 16384, 128
+ROW_TILES = BATCH // P
+GATES = 7 * D_H
+LSTM_GATES = 4 * D_H
+K_PASS = 4 * P
+PASSES = D_IN // K_PASS
+N_PASS = 512
+WINDOW_STARTS = (0, GATES - N_PASS)
+OVERLAP = 2 * N_PASS - GATES
+
+ROUND = 4
+ROUNDS = PASSES // ROUND
+ROUND_K = ROUND * K_PASS
+X_AHEAD = 4
+SCALE_GROUP = 8
+SMALL_STEP = ROUNDS - 3
+
+FLOPS = 2 * BATCH * D_IN * GATES + 2 * BATCH * D_H * GATES
+
+
+def tile_share_lstm_cell_pa_k_kernel(
+    tc,
+    x,
+    h_minors,
+    c_minors,
+    s0,
+    s1,
+    s2,
+    mask,
+    weight_ih_words,
+    weight_ih_scales,
+    bias_ih,
+    weight_hh,
+    bias_hh,
+    weight_sh0,
+    bias_sh0,
+    weight_sh1,
+    bias_sh1,
+    weight_sh2,
+    bias_sh2,
+    out_0,
+    out_1,
+    out_2,
+    out_3,
+    out_4,
+):
+    nc = tc.nc
+    with ExitStack() as stack:
+        stack.enter_context(tc.manual_schedule())
+        keep = stack.enter_context(tc.tile_pool(name="keep", bufs=1))
+        x_pool = stack.enter_context(tc.tile_pool(name="x_rows", bufs=X_AHEAD))
+        sorted_pool = stack.enter_context(tc.tile_pool(name="sorted", bufs=2))
+        grouped_pool = stack.enter_context(tc.tile_pool(name="grouped", bufs=ROUND))
+        codes_pool = stack.enter_context(tc.tile_pool(name="codes", bufs=2 * ROUND))
+        turn_psum = stack.enter_context(tc.psum_pool(name="turn", bufs=ROUND))
+        acc_psum = stack.enter_context(tc.psum_pool(name="acc", bufs=1))
+
+        w_planes = []
+        for group in range(PASSES // SCALE_GROUP):
+            planes = keep.tile([P, SCALE_GROUP, GATES], U8, name="w_planes%d" % group, align_bytes=64)
+            nc.vector.memset(planes[:].bitcast(I32), 0)
+            w_planes.append(planes)
+        w_words = [
+            keep.tile([P, ROUND, 2 * GATES], U8, name="w_words%d" % r, align_bytes=64) for r in range(ROUNDS)
+        ]
+
+        ident_f32 = keep.tile([P, P], F32, name="ident_f32")
+        make_identity(nc, ident_f32[:])
+        ident_bf16 = keep.tile([P, P], BF16, name="ident_bf16")
+        make_identity(nc, ident_bf16[:])
+        ones = keep.tile([P, P], BF16, name="ones")
+        nc.vector.memset(ones[:], 1.0)
+        bias_rows = keep.tile([P, GATES], BF16, name="bias_rows")
+        nc.vector.memset(bias_rows[:], 0.0)
+        mask_rows = keep.tile([P, P], BF16, name="mask_rows")
+        nc.vector.memset(mask_rows[:], 0.0)
+
+        table_in = keep.tile([P, 1], F32, name="table_in")
+        nc.vector.memset(table_in[:], 0.0)
+        table_out = keep.tile([P, 1], F32, name="table_out")
+        nc.scalar.activation(out=table_out[:], in_=table_in[:], func=ACT.Sigmoid)
+
+        acts = keep.tile([P, 4, ROW_TILES, D_H], BF16, name="acts")
+        for j, rows in enumerate((h_minors, s0, s1, s2)):
+            nc.gpsimd.dma_start(out=acts[:, j], in_=rows.rearrange("(rt p) d -> p rt d", p=P))
+        small_w = keep.tile([P, 7, D_H], BF16, name="small_w")
+        nc.gpsimd.dma_start(out=small_w[:, 0:4, :], in_=weight_hh.rearrange("(j p) d -> p j d", p=P))
+        for j, weight in enumerate((weight_sh0, weight_sh1, weight_sh2)):
+            nc.gpsimd.dma_start(out=small_w[:, 4 + j, :], in_=weight)
+        nc.gpsimd.dma_start(out=bias_rows[0:1, :], in_=bias_ih.rearrange("(o n) -> o n", o=1))
+        nc.gpsimd.dma_start(out=bias_rows[1:2, 0:LSTM_GATES], in_=bias_hh.rearrange("(o n) -> o n", o=1))
+        for j, bias in enumerate((bias_sh0, bias_sh1, bias_sh2)):
+            first = LSTM_GATES + j * D_H
+            nc.gpsimd.dma_start(out=bias_rows[1:2, first : first + D_H], in_=bias.rearrange("(o n) -> o n", o=1))
+        nc.gpsimd.dma_start(out=mask_rows[0:ROW_TILES, :], in_=mask.rearrange("(rt p) -> rt p", p=P))
+        c_rows = keep.tile([P, ROW_TILES, D_H], BF16, name="c_rows")
+        nc.gpsimd.dma_start(out=c_rows[:], in_=c_minors.rearrange("(rt p) d -> p rt d", p=P))
+
+        words_view = weight_ih_words.bitcast(I32)
+        scales_view = weight_ih_scales.bitcast(I32).rearrange("g (h q) n -> q h g n", h=2)
+        x_rows = {}
+        x_words = {}
+        x_codes = {}
+        x_planes = {}
+
+        def load_round(r):
+            x_rows[r] = x_pool.tile([P, ROW_TILES, ROUND_K], BF16, name="x_rows")
+            for rt in range(ROW_TILES):
+                nc.sync.dma_start(
+                    out=x_rows[r][:, rt, :], in_=x[rt * P : (rt + 1) * P, r * ROUND_K : (r + 1) * ROUND_K]
+                )
+            first_pass = r * ROUND
+            if first_pass % SCALE_GROUP == 0:
+                planes = w_planes[first_pass // SCALE_GROUP]
+                for q in range(8):
+                    partition = 32 * (q // 4) + q % 4
+                    nc.sync.dma_start(
+                        out=planes[partition:P:64, :, :].bitcast(I32),
+                        in_=scales_view[q, :, first_pass : first_pass + SCALE_GROUP, :],
+                    )
+            nc.sync.dma_start(
+                out=w_words[r][:].bitcast(I32),
+                in_=words_view[first_pass : first_pass + ROUND].rearrange("g p n -> p g n"),
+            )
+
+        def sort_round(r):
+            x_words[r] = sorted_pool.tile([P, ROW_TILES, ROUND, 2, P], F32, name="x_words")
+            for rt in range(ROW_TILES):
+                nc.vector.tensor_copy(
+                    out=x_words[r][:, rt],
+                    in_=x_rows[r][:, rt, :].bitcast(F32).rearrange("p (g w u) -> p g u w", g=ROUND, u=2),
+                )
+
+        def turn_and_quantise(r):
+            for i in range(ROUND):
+                turned = turn_psum.tile([P, ROW_TILES, 2, P], F32, name="turned", tag="bank")
+                for rt in range(ROW_TILES):
+                    for u in range(2):
+                        nc.tensor.transpose(turned[:, rt, u, :], x_words[r][:, rt, i, u, :], ident_f32[:])
+                grouped = grouped_pool.tile([P, 4 * BATCH], BF16, name="grouped", align_bytes=64)
+                nc.scalar.copy(
+                    out=grouped[:].bitcast(F32).rearrange("p (rt row u) -> p rt row u", rt=ROW_TILES, u=2),
+                    in_=turned[:].rearrange("p rt u row -> p rt row u"),
+                )
+                g = r * ROUND + i
+                x_codes[g] = codes_pool.tile([P, BATCH], U32, name="x_codes", align_bytes=64)
+                x_planes[g] = codes_pool.tile([P, BATCH], U8, name="x_planes", align_bytes=64)
+                nc.vector.quantize_mx(out=x_codes[g][:].bitcast(FP8X4), scales=x_planes[g][:], in_=grouped[:])
+
+        acc = [
+            [acc_psum.tile([P, N_PASS], F32, name="acc%d%d" % (window, rt)) for rt in range(ROW_TILES)]
+            for window in range(2)
+        ]
+
+        def multiply(window, rounds):
+            first = WINDOW_STARTS[window]
+            for r in rounds:
+                for rt in range(ROW_TILES):
+                    for i in range(ROUND):
+                        g = r * ROUND + i
+                        nc.tensor.matmul_mx(
+                            out=acc[window][rt][:],
+                            lhsT=x_codes[g][:, rt * P : (rt + 1) * P].bitcast(FP8X4),
+                            lhsT_scale=x_planes[g][:, rt * P : (rt + 1) * P],
+                            rhs=w_words[r][:, i, 2 * first : 2 * (first + N_PASS)].bitcast(FP4X4),
+                            rhs_scale=w_planes[g // SCALE_GROUP][:, g % SCALE_GROUP, first : first + N_PASS],
+                            start=(g == 0),
+                            stop=(g == PASSES - 1),
+                        )
+
+        acts_t = keep.tile([P, 4, ROW_TILES, P], BF16, name="acts_t")
+        small_w_t = keep.tile([P, GATES], BF16, name="small_w_t")
+        row_mask = keep.tile([P, ROW_TILES], F32, name="row_mask")
+        plain = keep.tile([P, ROW_TILES, GATES], F32, name="plain")
+
+        def small_transposes():
+            acts_bank = turn_psum.tile([P, 4, ROW_TILES, P], BF16, name="acts_bank", tag="bank")
+            for j in range(4):
+                for rt in range(ROW_TILES):
+                    nc.tensor.transpose(acts_bank[:, j, rt, :], acts[:, j, rt, :], ident_bf16[:])
+            nc.vector.tensor_copy(out=acts_t[:], in_=acts_bank[:])
+            w_bank = turn_psum.tile([P, 8, P], BF16, name="w_bank", tag="bank")
+            for j in range(7):
+                nc.tensor.transpose(w_bank[:, j, :], small_w[:, j, :], ident_bf16[:])
+            nc.tensor.transpose(w_bank[:, 7, :], mask_rows[:], ident_bf16[:])
+            nc.scalar.copy(out=small_w_t[:].rearrange("p (j n) -> p j n", j=7), in_=w_bank[:, 0:7, :])
+            nc.scalar.copy(out=row_mask[:], in_=w_bank[:, 7, 0:ROW_TILES])
+
+        def small_products():
+            for rt in range(ROW_TILES):
+                lstm_bank = turn_psum.tile([P, LSTM_GATES], F32, name="lstm_bank", tag="bank")
+                nc.tensor.matmul(
+                    lstm_bank[:], lhsT=acts_t[:, 0, rt, :], rhs=small_w_t[:, 0:LSTM_GATES], start=True, stop=False
+                )
+                nc.tensor.matmul(lstm_bank[:], lhsT=ones[:], rhs=bias_rows[:, 0:LSTM_GATES], start=False, stop=True)
+                nc.scalar.copy(out=plain[:, rt, 0:LSTM_GATES], in_=lstm_bank[:])
+                share_bank = turn_psum.tile([P, 3 * D_H], F32, name="share_bank", tag="bank")
+                nc.tensor.matmul(share_bank[:], lhsT=ones[:], rhs=bias_rows[:, LSTM_GATES:GATES], start=True, stop=False)
+                for j in range(3):
+                    nc.tensor.matmul(
+                        share_bank[:, j * D_H : (j + 1) * D_H],
+                        lhsT=acts_t[:, 1 + j, rt, :],
+                        rhs=small_w_t[:, LSTM_GATES + j * D_H : LSTM_GATES + (j + 1) * D_H],
+                        start=False,
+                        stop=(j == 2),
+                    )
+                nc.vector.tensor_copy(out=plain[:, rt, LSTM_GATES:GATES], in_=share_bank[:])
+
+        for r in range(X_AHEAD):
+            load_round(r)
+        for step in range(ROUNDS + 1):
+            if step < ROUNDS:
+                sort_round(step)
+            if step + X_AHEAD < ROUNDS:
+                load_round(step + X_AHEAD)
+            if step == SMALL_STEP:
+                small_transposes()
+            if step == SMALL_STEP + 1:
+                small_products()
+            if step >= 1:
+                turn_and_quantise(step - 1)
+            if 2 <= step < ROUNDS:
+                multiply(0, [step - 2])
+                multiply(1, [step - 2])
+
+        last_rounds = [ROUNDS - 2, ROUNDS - 1]
+        pre = keep.tile([P, ROW_TILES, GATES], F32, name="pre")
+        gate = keep.tile([P, ROW_TILES, GATES], F32, name="gate")
+        offset = keep.tile([P, ROW_TILES, 3, D_H], F32, name="offset")
+        tc_over = keep.tile([P, ROW_TILES, 3, D_H], F32, name="tc_over")
+        kept = keep.tile([P, ROW_TILES, D_H], F32, name="kept")
+        fresh = keep.tile([P, ROW_TILES, D_H], F32, name="fresh")
+        c_t = keep.tile([P, ROW_TILES, D_H], F32, name="c_t")
+        tanh_c = keep.tile([P, ROW_TILES, D_H], F32, name="tanh_c")
+        h_t = keep.tile([P, ROW_TILES, D_H], F32, name="h_t")
+        both = range(ROW_TILES)
+
+        def store(result, out):
+            nc.sync.dma_start(out=out.rearrange("(rt p) d -> p rt d", p=P), in_=result[:])
+
+        multiply(0, last_rounds)
+        for rt in both:
+            nc.vector.tensor_tensor(
+                out=pre[:, rt, 0:LSTM_GATES], in0=acc[0][rt][:], in1=plain[:, rt, 0:LSTM_GATES], op=ALU.add
+            )
+            nc.scalar.activation(out=gate[:, rt, 0 : 3 * D_H], in_=pre[:, rt, 0 : 3 * D_H], func=ACT.Sigmoid)
+            nc.scalar.activation(
+                out=gate[:, rt, 3 * D_H : LSTM_GATES], in_=pre[:, rt, 3 * D_H : LSTM_GATES], func=ACT.Tanh
+            )
+        in_gate = [gate[:, rt, 0:D_H] for rt in both]
+        forget_gate = [gate[:, rt, D_H : 2 * D_H] for rt in both]
+        out_gate = [gate[:, rt, 2 * D_H : 3 * D_H] for rt in both]
+        candidate = [gate[:, rt, 3 * D_H : LSTM_GATES] for rt in both]
+        m = [row_mask[:, rt : rt + 1] for rt in both]
+        for rt in both:
+            nc.vector.scalar_tensor_tensor(
+                out=kept[:, rt, :], in0=forget_gate[rt], scalar=m[rt], in1=c_rows[:, rt, :], op0=ALU.mult, op1=ALU.mult
+            )
+        for rt in both:
+            nc.vector.scalar_tensor_tensor(
+                out=fresh[:, rt, :], in0=in_gate[rt], scalar=m[rt], in1=candidate[rt], op0=ALU.mult, op1=ALU.mult
+            )
+        for rt in both:
+            nc.vector.tensor_tensor(out=c_t[:, rt, :], in0=kept[:, rt, :], in1=fresh[:, rt, :], op=ALU.add)
+        store(c_t, out_1)
+        for rt in both:
+            for j in range(3):
+                nc.scalar.activation(
+                    out=offset[:, rt, j, :], in_=out_gate[rt], func=ACT.Copy, bias=float(j + 1), scale=-1.0
+                )
+        for rt in both:
+            nc.scalar.activation(out=tanh_c[:, rt, :], in_=c_t[:, rt, :], func=ACT.Tanh)
+            nc.scalar.activation(out=tc_over[:, rt, 0, :], in_=tanh_c[:, rt, :], func=ACT.Copy, scale=m[rt])
+        for rt in both:
+            nc.vector.tensor_tensor(out=h_t[:, rt, :], in0=out_gate[rt], in1=tc_over[:, rt, 0, :], op=ALU.mult)
+            for j in (1, 2):
+                nc.scalar.activation(
+                    out=tc_over[:, rt, j, :], in_=tc_over[:, rt, 0, :], func=ACT.Copy, scale=1.0 / (j + 1)
+                )
+        store(h_t, out_0)
+
+        multiply(1, last_rounds)
+        rest = keep.tile([P, ROW_TILES, 3, D_H], F32, name="rest")
+        s_0 = keep.tile([P, ROW_TILES, D_H], F32, name="s_0")
+        s_1 = keep.tile([P, ROW_TILES, D_H], F32, name="s_1")
+        s_2 = keep.tile([P, ROW_TILES, D_H], F32, name="s_2")
+        rest_1 = keep.tile([P, ROW_TILES, D_H], F32, name="rest_1")
+        taken_2 = keep.tile([P, ROW_TILES, D_H], F32, name="taken_2")
+        rest_2 = keep.tile([P, ROW_TILES, D_H], F32, name="rest_2")
+        for rt in both:
+            nc.vector.tensor_tensor(
+                out=pre[:, rt, LSTM_GATES:GATES],
+                in0=acc[1][rt][:, OVERLAP:N_PASS],
+                in1=plain[:, rt, LSTM_GATES:GATES],
+                op=ALU.add,
+            )
+            nc.scalar.activation(out=gate[:, rt, LSTM_GATES:GATES], in_=pre[:, rt, LSTM_GATES:GATES], func=ACT.Sigmoid)
+        for rt in both:
+            nc.vector.tensor_tensor(
+                out=rest[:, rt].rearrange("p j d -> p (j d)"),
+                in0=gate[:, rt, LSTM_GATES:GATES],
+                in1=offset[:, rt].rearrange("p j d -> p (j d)"),
+                op=ALU.add,
+            )
+        for rt in both:
+            nc.vector.tensor_tensor(out=s_0[:, rt, :], in0=rest[:, rt, 0, :], in1=tc_over[:, rt, 0, :], op=ALU.mult)
+        store(s_0, out_2)
+        for rt in both:
+            nc.vector.tensor_tensor(out=rest_1[:, rt, :], in0=rest[:, rt, 1, :], in1=s_0[:, rt, :], op=ALU.subtract)
+        for rt in both:
+            nc.vector.tensor_tensor(out=s_1[:, rt, :], in0=rest_1[:, rt, :], in1=tc_over[:, rt, 1, :], op=ALU.mult)
+        store(s_1, out_3)
+        for rt in both:
+            nc.vector.scalar_tensor_tensor(
+                out=taken_2[:, rt, :], in0=s_0[:, rt, :], scalar=2.0, in1=s_1[:, rt, :], op0=ALU.mult, op1=ALU.add
+            )
+        for rt in both:
+            nc.vector.tensor_tensor(out=rest_2[:, rt, :], in0=rest[:, rt, 2, :], in1=taken_2[:, rt, :], op=ALU.subtract)
+        for rt in both:
+            nc.vector.tensor_tensor(out=s_2[:, rt, :], in0=rest_2[:, rt, :], in1=tc_over[:, rt, 2, :], op=ALU.mult)
+        store(s_2, out_4)

@@ -25,11 +25,8 @@ WINDOW_STARTS = (0, GATES - N_PASS)
 OVERLAP = 2 * N_PASS - GATES
 
 ROUND = 4
-ROUNDS = PASSES // ROUND
-ROUND_K = ROUND * K_PASS
 X_AHEAD = 4
 SCALE_GROUP = 8
-SMALL_STEP = ROUNDS - 3
 
 FLOPS = 2 * BATCH * D_IN * GATES + 2 * BATCH * D_H * GATES
 
@@ -71,14 +68,14 @@ def tile_share_lstm_cell_pa_k_kernel(
         turn_psum = stack.enter_context(tc.psum_pool(name="turn", bufs=ROUND))
         acc_psum = stack.enter_context(tc.psum_pool(name="acc", bufs=1))
 
-        w_planes = []
-        for group in range(PASSES // SCALE_GROUP):
-            planes = keep.tile([P, SCALE_GROUP, GATES], U8, name="w_planes%d" % group, align_bytes=64)
-            nc.vector.memset(planes[:].bitcast(I32), 0)
-            w_planes.append(planes)
-        w_words = [
-            keep.tile([P, ROUND, 2 * GATES], U8, name="w_words%d" % r, align_bytes=64) for r in range(ROUNDS)
-        ]
+        rounds = []
+        first_pass = 0
+        while first_pass < PASSES:
+            size = min(max(first_pass, 1), ROUND)
+            rounds.append((first_pass, size))
+            first_pass += size
+        n_rounds = len(rounds)
+        small_step = n_rounds - 2
 
         ident_f32 = keep.tile([P, P], F32, name="ident_f32")
         make_identity(nc, ident_f32[:])
@@ -114,41 +111,52 @@ def tile_share_lstm_cell_pa_k_kernel(
 
         words_view = weight_ih_words.bitcast(I32)
         scales_view = weight_ih_scales.bitcast(I32).rearrange("g (h q) n -> q h g n", h=2)
+        w_planes = {}
+        w_words = {}
         x_rows = {}
         x_words = {}
         x_codes = {}
         x_planes = {}
 
-        def load_round(r):
-            x_rows[r] = x_pool.tile([P, ROW_TILES, ROUND_K], BF16, name="x_rows")
+        def load_x(r):
+            first, size = rounds[r]
+            x_rows[r] = x_pool.tile([P, ROW_TILES, size * K_PASS], BF16, name="x_rows")
             for rt in range(ROW_TILES):
                 nc.sync.dma_start(
-                    out=x_rows[r][:, rt, :], in_=x[rt * P : (rt + 1) * P, r * ROUND_K : (r + 1) * ROUND_K]
+                    out=x_rows[r][:, rt, :], in_=x[rt * P : (rt + 1) * P, first * K_PASS : (first + size) * K_PASS]
                 )
-            first_pass = r * ROUND
-            if first_pass % SCALE_GROUP == 0:
-                planes = w_planes[first_pass // SCALE_GROUP]
+
+        def load_w(r):
+            first, size = rounds[r]
+            if first % SCALE_GROUP == 0:
+                group = first // SCALE_GROUP
+                planes = keep.tile([P, SCALE_GROUP, GATES], U8, name="w_planes%d" % group, align_bytes=64)
+                nc.vector.memset(planes[:].bitcast(I32), 0)
                 for q in range(8):
                     partition = 32 * (q // 4) + q % 4
                     nc.sync.dma_start(
                         out=planes[partition:P:64, :, :].bitcast(I32),
-                        in_=scales_view[q, :, first_pass : first_pass + SCALE_GROUP, :],
+                        in_=scales_view[q, :, first : first + SCALE_GROUP, :],
                     )
+                w_planes[group] = planes
+            w_words[r] = keep.tile([P, size, 2 * GATES], U8, name="w_words%d" % r, align_bytes=64)
             nc.sync.dma_start(
                 out=w_words[r][:].bitcast(I32),
-                in_=words_view[first_pass : first_pass + ROUND].rearrange("g p n -> p g n"),
+                in_=words_view[first : first + size].rearrange("g p n -> p g n"),
             )
 
         def sort_round(r):
-            x_words[r] = sorted_pool.tile([P, ROW_TILES, ROUND, 2, P], F32, name="x_words")
+            size = rounds[r][1]
+            x_words[r] = sorted_pool.tile([P, ROW_TILES, size, 2, P], F32, name="x_words")
             for rt in range(ROW_TILES):
                 nc.vector.tensor_copy(
                     out=x_words[r][:, rt],
-                    in_=x_rows[r][:, rt, :].bitcast(F32).rearrange("p (g w u) -> p g u w", g=ROUND, u=2),
+                    in_=x_rows[r][:, rt, :].bitcast(F32).rearrange("p (g w u) -> p g u w", g=size, u=2),
                 )
 
         def turn_and_quantise(r):
-            for i in range(ROUND):
+            first, size = rounds[r]
+            for i in range(size):
                 turned = turn_psum.tile([P, ROW_TILES, 2, P], F32, name="turned", tag="bank")
                 for rt in range(ROW_TILES):
                     for u in range(2):
@@ -158,7 +166,7 @@ def tile_share_lstm_cell_pa_k_kernel(
                     out=grouped[:].bitcast(F32).rearrange("p (rt row u) -> p rt row u", rt=ROW_TILES, u=2),
                     in_=turned[:].rearrange("p rt u row -> p rt row u"),
                 )
-                g = r * ROUND + i
+                g = first + i
                 x_codes[g] = codes_pool.tile([P, BATCH], U32, name="x_codes", align_bytes=64)
                 x_planes[g] = codes_pool.tile([P, BATCH], U8, name="x_planes", align_bytes=64)
                 nc.vector.quantize_mx(out=x_codes[g][:].bitcast(FP8X4), scales=x_planes[g][:], in_=grouped[:])
@@ -168,18 +176,19 @@ def tile_share_lstm_cell_pa_k_kernel(
             for window in range(2)
         ]
 
-        def multiply(window, rounds):
-            first = WINDOW_STARTS[window]
-            for r in rounds:
+        def multiply(window, which_rounds):
+            column = WINDOW_STARTS[window]
+            for r in which_rounds:
+                first, size = rounds[r]
                 for rt in range(ROW_TILES):
-                    for i in range(ROUND):
-                        g = r * ROUND + i
+                    for i in range(size):
+                        g = first + i
                         nc.tensor.matmul_mx(
                             out=acc[window][rt][:],
                             lhsT=x_codes[g][:, rt * P : (rt + 1) * P].bitcast(FP8X4),
                             lhsT_scale=x_planes[g][:, rt * P : (rt + 1) * P],
-                            rhs=w_words[r][:, i, 2 * first : 2 * (first + N_PASS)].bitcast(FP4X4),
-                            rhs_scale=w_planes[g // SCALE_GROUP][:, g % SCALE_GROUP, first : first + N_PASS],
+                            rhs=w_words[r][:, i, 2 * column : 2 * (column + N_PASS)].bitcast(FP4X4),
+                            rhs_scale=w_planes[g // SCALE_GROUP][:, g % SCALE_GROUP, column : column + N_PASS],
                             start=(g == 0),
                             stop=(g == PASSES - 1),
                         )
@@ -222,24 +231,28 @@ def tile_share_lstm_cell_pa_k_kernel(
                     )
                 nc.vector.tensor_copy(out=plain[:, rt, LSTM_GATES:GATES], in_=share_bank[:])
 
-        for r in range(X_AHEAD):
-            load_round(r)
-        for step in range(ROUNDS + 1):
-            if step < ROUNDS:
+        load_x(0)
+        for r in range(1, X_AHEAD):
+            load_x(r)
+            load_w(r - 1)
+        for step in range(n_rounds + 1):
+            if step < n_rounds:
                 sort_round(step)
-            if step + X_AHEAD < ROUNDS:
-                load_round(step + X_AHEAD)
-            if step == SMALL_STEP:
+            if step + X_AHEAD < n_rounds:
+                load_x(step + X_AHEAD)
+            if step + X_AHEAD - 1 < n_rounds:
+                load_w(step + X_AHEAD - 1)
+            if step == small_step:
                 small_transposes()
-            if step == SMALL_STEP + 1:
+            if step == small_step + 1:
                 small_products()
             if step >= 1:
                 turn_and_quantise(step - 1)
-            if 2 <= step < ROUNDS:
+            if 2 <= step < n_rounds:
                 multiply(0, [step - 2])
                 multiply(1, [step - 2])
 
-        last_rounds = [ROUNDS - 2, ROUNDS - 1]
+        last_rounds = [n_rounds - 2, n_rounds - 1]
         pre = keep.tile([P, ROW_TILES, GATES], F32, name="pre")
         gate = keep.tile([P, ROW_TILES, GATES], F32, name="gate")
         offset = keep.tile([P, ROW_TILES, 3, D_H], F32, name="offset")

@@ -20,9 +20,10 @@ GATES = 7 * D_H
 LSTM_GATES = 4 * D_H
 K_PASS = 4 * P
 PASSES = D_IN // K_PASS
-N_PASS = 512
-WINDOW_STARTS = (0, GATES - N_PASS)
-OVERLAP = 2 * N_PASS - GATES
+WINDOWS = (
+    ((0, LSTM_GATES),),
+    ((LSTM_GATES, D_H), (LSTM_GATES + D_H, D_H), (LSTM_GATES + 2 * D_H, D_H)),
+)
 
 ROUND = 4
 X_AHEAD = 4
@@ -172,26 +173,28 @@ def tile_share_lstm_cell_pa_k_kernel(
                 nc.vector.quantize_mx(out=x_codes[g][:].bitcast(FP8X4), scales=x_planes[g][:], in_=grouped[:])
 
         acc = [
-            [acc_psum.tile([P, N_PASS], F32, name="acc%d%d" % (window, rt)) for rt in range(ROW_TILES)]
+            [acc_psum.tile([P, LSTM_GATES], F32, name="acc%d%d" % (window, rt)) for rt in range(ROW_TILES)]
             for window in range(2)
         ]
 
         def multiply(window, which_rounds):
-            column = WINDOW_STARTS[window]
+            pieces = WINDOWS[window]
             for r in which_rounds:
                 first, size = rounds[r]
                 for rt in range(ROW_TILES):
                     for i in range(size):
                         g = first + i
-                        nc.tensor.matmul_mx(
-                            out=acc[window][rt][:],
-                            lhsT=x_codes[g][:, rt * P : (rt + 1) * P].bitcast(FP8X4),
-                            lhsT_scale=x_planes[g][:, rt * P : (rt + 1) * P],
-                            rhs=w_words[r][:, i, 2 * column : 2 * (column + N_PASS)].bitcast(FP4X4),
-                            rhs_scale=w_planes[g // SCALE_GROUP][:, g % SCALE_GROUP, column : column + N_PASS],
-                            start=(g == 0),
-                            stop=(g == PASSES - 1),
-                        )
+                        for n, (column, width) in enumerate(pieces):
+                            in_bank = column - pieces[0][0]
+                            nc.tensor.matmul_mx(
+                                out=acc[window][rt][:, in_bank : in_bank + width],
+                                lhsT=x_codes[g][:, rt * P : (rt + 1) * P].bitcast(FP8X4),
+                                lhsT_scale=x_planes[g][:, rt * P : (rt + 1) * P],
+                                rhs=w_words[r][:, i, 2 * column : 2 * (column + width)].bitcast(FP4X4),
+                                rhs_scale=w_planes[g // SCALE_GROUP][:, g % SCALE_GROUP, column : column + width],
+                                start=(g == 0 and n == 0),
+                                stop=(g == PASSES - 1 and n == len(pieces) - 1),
+                            )
 
         acts_t = keep.tile([P, 4, ROW_TILES, P], BF16, name="acts_t")
         small_w_t = keep.tile([P, GATES], BF16, name="small_w_t")
@@ -319,7 +322,7 @@ def tile_share_lstm_cell_pa_k_kernel(
         for rt in both:
             nc.vector.tensor_tensor(
                 out=pre[:, rt, LSTM_GATES:GATES],
-                in0=acc[1][rt][:, OVERLAP:N_PASS],
+                in0=acc[1][rt][:, 0 : 3 * D_H],
                 in1=plain[:, rt, LSTM_GATES:GATES],
                 op=ALU.add,
             )

@@ -65,7 +65,7 @@ def tile_share_lstm_cell_pa_k_kernel(
         x_pool = stack.enter_context(tc.tile_pool(name="x_rows", bufs=X_AHEAD))
         sorted_pool = stack.enter_context(tc.tile_pool(name="sorted", bufs=2))
         grouped_pool = stack.enter_context(tc.tile_pool(name="grouped", bufs=ROUND))
-        codes_pool = stack.enter_context(tc.tile_pool(name="codes", bufs=2 * ROUND))
+        codes_pool = stack.enter_context(tc.tile_pool(name="codes", bufs=4 * ROUND))
         turn_psum = stack.enter_context(tc.psum_pool(name="turn", bufs=ROUND))
         acc_psum = stack.enter_context(tc.psum_pool(name="acc", bufs=1))
 
@@ -76,7 +76,9 @@ def tile_share_lstm_cell_pa_k_kernel(
             rounds.append((first_pass, size))
             first_pass += size
         n_rounds = len(rounds)
-        small_step = n_rounds - 2
+        small_step = n_rounds - 3
+        late_lstm = n_rounds - 2
+        late_shared = n_rounds - 3
 
         ident_f32 = keep.tile([P, P], F32, name="ident_f32")
         make_identity(nc, ident_f32[:])
@@ -173,28 +175,28 @@ def tile_share_lstm_cell_pa_k_kernel(
                 nc.vector.quantize_mx(out=x_codes[g][:].bitcast(FP8X4), scales=x_planes[g][:], in_=grouped[:])
 
         acc = [
-            [acc_psum.tile([P, LSTM_GATES], F32, name="acc%d%d" % (window, rt)) for rt in range(ROW_TILES)]
+            [
+                acc_psum.tile([P, LSTM_GATES], F32, name="acc%d%d" % (window, rt), tag="acc%d%d" % (window, rt))
+                for rt in range(ROW_TILES)
+            ]
             for window in range(2)
         ]
 
-        def multiply(window, which_rounds):
-            pieces = WINDOWS[window]
-            for r in which_rounds:
-                first, size = rounds[r]
-                for rt in range(ROW_TILES):
-                    for i in range(size):
-                        g = first + i
-                        for n, (column, width) in enumerate(pieces):
-                            in_bank = column - pieces[0][0]
-                            nc.tensor.matmul_mx(
-                                out=acc[window][rt][:, in_bank : in_bank + width],
-                                lhsT=x_codes[g][:, rt * P : (rt + 1) * P].bitcast(FP8X4),
-                                lhsT_scale=x_planes[g][:, rt * P : (rt + 1) * P],
-                                rhs=w_words[r][:, i, 2 * column : 2 * (column + width)].bitcast(FP4X4),
-                                rhs_scale=w_planes[g // SCALE_GROUP][:, g % SCALE_GROUP, column : column + width],
-                                start=(g == 0 and n == 0),
-                                stop=(g == PASSES - 1 and n == len(pieces) - 1),
-                            )
+        def multiply(bank, rt, pieces, r, first_round, last_round):
+            first, size = rounds[r]
+            for i in range(size):
+                g = first + i
+                for n, (column, width) in enumerate(pieces):
+                    in_bank = column - pieces[0][0]
+                    nc.tensor.matmul_mx(
+                        out=bank[:, in_bank : in_bank + width],
+                        lhsT=x_codes[g][:, rt * P : (rt + 1) * P].bitcast(FP8X4),
+                        lhsT_scale=x_planes[g][:, rt * P : (rt + 1) * P],
+                        rhs=w_words[r][:, i, 2 * column : 2 * (column + width)].bitcast(FP4X4),
+                        rhs_scale=w_planes[g // SCALE_GROUP][:, g % SCALE_GROUP, column : column + width],
+                        start=(r == first_round and i == 0 and n == 0),
+                        stop=(r == last_round and i == size - 1 and n == len(pieces) - 1),
+                    )
 
         acts_t = keep.tile([P, 4, ROW_TILES, P], BF16, name="acts_t")
         small_w_t = keep.tile([P, GATES], BF16, name="small_w_t")
@@ -251,103 +253,137 @@ def tile_share_lstm_cell_pa_k_kernel(
                 small_products()
             if step >= 1:
                 turn_and_quantise(step - 1)
-            if 2 <= step < n_rounds:
-                multiply(0, [step - 2])
-                multiply(1, [step - 2])
+            r = step - 2
+            if 0 <= r < late_lstm:
+                for rt in range(ROW_TILES):
+                    multiply(acc[0][rt], rt, WINDOWS[0], r, 0, n_rounds - 1)
+            if 0 <= r < late_shared:
+                for rt in range(ROW_TILES):
+                    multiply(acc[1][rt], rt, WINDOWS[1], r, 0, late_shared - 1)
 
-        last_rounds = [n_rounds - 2, n_rounds - 1]
-        pre = keep.tile([P, ROW_TILES, GATES], F32, name="pre")
-        gate = keep.tile([P, ROW_TILES, GATES], F32, name="gate")
-        offset = keep.tile([P, ROW_TILES, 3, D_H], F32, name="offset")
-        tc_over = keep.tile([P, ROW_TILES, 3, D_H], F32, name="tc_over")
-        kept = keep.tile([P, ROW_TILES, D_H], F32, name="kept")
-        fresh = keep.tile([P, ROW_TILES, D_H], F32, name="fresh")
-        c_t = keep.tile([P, ROW_TILES, D_H], F32, name="c_t")
-        tanh_c = keep.tile([P, ROW_TILES, D_H], F32, name="tanh_c")
-        h_t = keep.tile([P, ROW_TILES, D_H], F32, name="h_t")
         both = range(ROW_TILES)
-
-        def store(result, out):
-            nc.sync.dma_start(out=out.rearrange("(rt p) d -> p rt d", p=P), in_=result[:])
-
-        multiply(0, last_rounds)
-        for rt in both:
-            nc.vector.tensor_tensor(
-                out=pre[:, rt, 0:LSTM_GATES], in0=acc[0][rt][:], in1=plain[:, rt, 0:LSTM_GATES], op=ALU.add
-            )
-            nc.scalar.activation(out=gate[:, rt, 0 : 3 * D_H], in_=pre[:, rt, 0 : 3 * D_H], func=ACT.Sigmoid)
-            nc.scalar.activation(
-                out=gate[:, rt, 3 * D_H : LSTM_GATES], in_=pre[:, rt, 3 * D_H : LSTM_GATES], func=ACT.Tanh
-            )
+        pre = keep.tile([P, ROW_TILES, LSTM_GATES], F32, name="pre")
+        gate = keep.tile([P, ROW_TILES, LSTM_GATES], F32, name="gate")
+        base = keep.tile([P, ROW_TILES, 3 * D_H], F32, name="base")
+        pre_b = [[keep.tile([P, D_H], F32, name="pre_b%d%d" % (j, rt)) for rt in both] for j in range(3)]
+        share = [[keep.tile([P, D_H], F32, name="share%d%d" % (j, rt)) for rt in both] for j in range(3)]
+        kept = [keep.tile([P, D_H], F32, name="kept%d" % rt) for rt in both]
+        fresh = [keep.tile([P, D_H], F32, name="fresh%d" % rt) for rt in both]
+        tanh_c = [keep.tile([P, D_H], F32, name="tanh_c%d" % rt) for rt in both]
+        tc_t = [keep.tile([P, D_H], F32, name="tc_t%d" % rt) for rt in both]
+        taken = [[keep.tile([P, D_H], F32, name="taken%d%d" % (j, rt)) for rt in both] for j in range(3)]
+        rest = [[keep.tile([P, D_H], F32, name="rest%d%d" % (j, rt)) for rt in both] for j in range(3)]
+        c_t = keep.tile([P, ROW_TILES, D_H], F32, name="c_t")
+        h_t = keep.tile([P, ROW_TILES, D_H], F32, name="h_t")
+        s_t = [keep.tile([P, ROW_TILES, D_H], F32, name="s_t%d" % j) for j in range(3)]
         in_gate = [gate[:, rt, 0:D_H] for rt in both]
         forget_gate = [gate[:, rt, D_H : 2 * D_H] for rt in both]
         out_gate = [gate[:, rt, 2 * D_H : 3 * D_H] for rt in both]
         candidate = [gate[:, rt, 3 * D_H : LSTM_GATES] for rt in both]
         m = [row_mask[:, rt : rt + 1] for rt in both]
-        for rt in both:
-            nc.vector.scalar_tensor_tensor(
-                out=kept[:, rt, :], in0=forget_gate[rt], scalar=m[rt], in1=c_rows[:, rt, :], op0=ALU.mult, op1=ALU.mult
-            )
-        for rt in both:
-            nc.vector.scalar_tensor_tensor(
-                out=fresh[:, rt, :], in0=in_gate[rt], scalar=m[rt], in1=candidate[rt], op0=ALU.mult, op1=ALU.mult
-            )
-        for rt in both:
-            nc.vector.tensor_tensor(out=c_t[:, rt, :], in0=kept[:, rt, :], in1=fresh[:, rt, :], op=ALU.add)
-        store(c_t, out_1)
-        for rt in both:
-            for j in range(3):
-                nc.scalar.activation(
-                    out=offset[:, rt, j, :], in_=out_gate[rt], func=ACT.Copy, bias=float(j + 1), scale=-1.0
-                )
-        for rt in both:
-            nc.scalar.activation(out=tanh_c[:, rt, :], in_=c_t[:, rt, :], func=ACT.Tanh)
-            nc.scalar.activation(out=tc_over[:, rt, 0, :], in_=tanh_c[:, rt, :], func=ACT.Copy, scale=m[rt])
-        for rt in both:
-            nc.vector.tensor_tensor(out=h_t[:, rt, :], in0=out_gate[rt], in1=tc_over[:, rt, 0, :], op=ALU.mult)
-            for j in (1, 2):
-                nc.scalar.activation(
-                    out=tc_over[:, rt, j, :], in_=tc_over[:, rt, 0, :], func=ACT.Copy, scale=1.0 / (j + 1)
-                )
-        store(h_t, out_0)
 
-        multiply(1, last_rounds)
-        rest = keep.tile([P, ROW_TILES, 3, D_H], F32, name="rest")
-        s_0 = keep.tile([P, ROW_TILES, D_H], F32, name="s_0")
-        s_1 = keep.tile([P, ROW_TILES, D_H], F32, name="s_1")
-        s_2 = keep.tile([P, ROW_TILES, D_H], F32, name="s_2")
-        rest_1 = keep.tile([P, ROW_TILES, D_H], F32, name="rest_1")
-        taken_2 = keep.tile([P, ROW_TILES, D_H], F32, name="taken_2")
-        rest_2 = keep.tile([P, ROW_TILES, D_H], F32, name="rest_2")
-        for rt in both:
-            nc.vector.tensor_tensor(
-                out=pre[:, rt, LSTM_GATES:GATES],
-                in0=acc[1][rt][:, 0 : 3 * D_H],
-                in1=plain[:, rt, LSTM_GATES:GATES],
-                op=ALU.add,
-            )
-            nc.scalar.activation(out=gate[:, rt, LSTM_GATES:GATES], in_=pre[:, rt, LSTM_GATES:GATES], func=ACT.Sigmoid)
-        for rt in both:
-            nc.vector.tensor_tensor(
-                out=rest[:, rt].rearrange("p j d -> p (j d)"),
-                in0=gate[:, rt, LSTM_GATES:GATES],
-                in1=offset[:, rt].rearrange("p j d -> p (j d)"),
-                op=ALU.add,
-            )
-        for rt in both:
-            nc.vector.tensor_tensor(out=s_0[:, rt, :], in0=rest[:, rt, 0, :], in1=tc_over[:, rt, 0, :], op=ALU.mult)
-        store(s_0, out_2)
-        for rt in both:
-            nc.vector.tensor_tensor(out=rest_1[:, rt, :], in0=rest[:, rt, 1, :], in1=s_0[:, rt, :], op=ALU.subtract)
-        for rt in both:
-            nc.vector.tensor_tensor(out=s_1[:, rt, :], in0=rest_1[:, rt, :], in1=tc_over[:, rt, 1, :], op=ALU.mult)
-        store(s_1, out_3)
-        for rt in both:
+        def store(result, out):
+            nc.sync.dma_start(out=out.rearrange("(rt p) d -> p rt d", p=P), in_=result[:])
+
+        def gates(rt):
+            nc.vector.tensor_tensor(out=pre[:, rt, :], in0=acc[0][rt][:], in1=plain[:, rt, 0:LSTM_GATES], op=ALU.add)
+            nc.scalar.activation(out=gate[:, rt, 0 : 3 * D_H], in_=pre[:, rt, 0 : 3 * D_H], func=ACT.Sigmoid)
+            nc.scalar.activation(out=candidate[rt], in_=pre[:, rt, 3 * D_H : LSTM_GATES], func=ACT.Tanh)
+
+        def cell(rt):
             nc.vector.scalar_tensor_tensor(
-                out=taken_2[:, rt, :], in0=s_0[:, rt, :], scalar=2.0, in1=s_1[:, rt, :], op0=ALU.mult, op1=ALU.add
+                out=kept[rt][:], in0=forget_gate[rt], scalar=m[rt], in1=c_rows[:, rt, :], op0=ALU.mult, op1=ALU.mult
+            )
+            nc.vector.scalar_tensor_tensor(
+                out=fresh[rt][:], in0=in_gate[rt], scalar=m[rt], in1=candidate[rt], op0=ALU.mult, op1=ALU.mult
+            )
+            nc.vector.tensor_tensor(out=c_t[:, rt, :], in0=kept[rt][:], in1=fresh[rt][:], op=ALU.add)
+            nc.scalar.activation(out=tanh_c[rt][:], in_=c_t[:, rt, :], func=ACT.Tanh)
+
+        def hidden(rt):
+            nc.vector.tensor_scalar(out=tc_t[rt][:], in0=tanh_c[rt][:], scalar1=m[rt], scalar2=None, op0=ALU.mult)
+            nc.vector.scalar_tensor_tensor(
+                out=h_t[:, rt, :], in0=tanh_c[rt][:], scalar=m[rt], in1=out_gate[rt], op0=ALU.mult, op1=ALU.mult
+            )
+
+        def shared_sum(j, rt):
+            if j == 0:
+                bank = acc_psum.tile([P, LSTM_GATES], F32, name="late_b0", tag="acc1%d" % rt)
+            else:
+                bank = turn_psum.tile([P, LSTM_GATES], F32, name="late_b", tag="bank")
+            for r in range(late_shared, n_rounds):
+                multiply(bank, rt, WINDOWS[1][j : j + 1], r, late_shared, n_rounds - 1)
+            return bank
+
+        def shared_gate(j, rt, bank):
+            nc.vector.tensor_tensor(
+                out=pre_b[j][rt][:], in0=bank[:, 0:D_H], in1=base[:, rt, j * D_H : (j + 1) * D_H], op=ALU.add
+            )
+            nc.scalar.activation(out=share[j][rt][:], in_=pre_b[j][rt][:], func=ACT.Sigmoid)
+
+        def state(j, rt):
+            if j == 0:
+                subtracted = out_gate[rt]
+            else:
+                subtracted = taken[j][rt][:]
+            nc.vector.scalar_tensor_tensor(
+                out=rest[j][rt][:],
+                in0=share[j][rt][:],
+                scalar=float(j + 1),
+                in1=subtracted,
+                op0=ALU.add,
+                op1=ALU.subtract,
+            )
+            nc.vector.scalar_tensor_tensor(
+                out=s_t[j][:, rt, :],
+                in0=rest[j][rt][:],
+                scalar=1.0 / (j + 1),
+                in1=tc_t[rt][:],
+                op0=ALU.mult,
+                op1=ALU.mult,
+            )
+
+        def take_1(rt):
+            nc.vector.tensor_tensor(out=taken[1][rt][:], in0=out_gate[rt], in1=s_t[0][:, rt, :], op=ALU.add)
+            nc.vector.tensor_tensor(out=taken[0][rt][:], in0=taken[1][rt][:], in1=s_t[0][:, rt, :], op=ALU.add)
+
+        def take_2(rt):
+            nc.vector.tensor_tensor(out=taken[2][rt][:], in0=taken[0][rt][:], in1=s_t[1][:, rt, :], op=ALU.add)
+
+        for rt in both:
+            nc.vector.tensor_tensor(
+                out=base[:, rt, :], in0=acc[1][rt][:, 0 : 3 * D_H], in1=plain[:, rt, LSTM_GATES:GATES], op=ALU.add
             )
         for rt in both:
-            nc.vector.tensor_tensor(out=rest_2[:, rt, :], in0=rest[:, rt, 2, :], in1=taken_2[:, rt, :], op=ALU.subtract)
-        for rt in both:
-            nc.vector.tensor_tensor(out=s_2[:, rt, :], in0=rest_2[:, rt, :], in1=tc_over[:, rt, 2, :], op=ALU.mult)
-        store(s_2, out_4)
+            for r in range(late_lstm, n_rounds):
+                multiply(acc[0][rt], rt, WINDOWS[0], r, 0, n_rounds - 1)
+        late = [[shared_sum(j, rt) for rt in both] for j in range(3)]
+
+        gates(0)
+        cell(0)
+        gates(1)
+        hidden(0)
+        shared_gate(0, 0, late[0][0])
+        cell(1)
+        store(c_t, out_1)
+        shared_gate(0, 1, late[0][1])
+        state(0, 0)
+        hidden(1)
+        store(h_t, out_0)
+        take_1(0)
+        state(0, 1)
+        store(s_t[0], out_2)
+        shared_gate(1, 0, late[1][0])
+        take_1(1)
+        state(1, 0)
+        shared_gate(1, 1, late[1][1])
+        take_2(0)
+        state(1, 1)
+        store(s_t[1], out_3)
+        shared_gate(2, 0, late[2][0])
+        take_2(1)
+        state(2, 0)
+        nc.sync.dma_start(out=out_4[0:P, :], in_=s_t[2][:, 0, :])
+        shared_gate(2, 1, late[2][1])
+        state(2, 1)
+        nc.sync.dma_start(out=out_4[P:BATCH, :], in_=s_t[2][:, 1, :])

@@ -27,7 +27,7 @@ WINDOWS = (
 
 ROUND = 4
 X_AHEAD = 4
-SCALE_GROUP = 8
+SCALE_GROUP = ROUND
 
 FLOPS = 2 * BATCH * D_IN * GATES + 2 * BATCH * D_H * GATES
 
@@ -65,7 +65,7 @@ def tile_share_lstm_cell_pa_k_kernel(
         x_pool = stack.enter_context(tc.tile_pool(name="x_rows", bufs=X_AHEAD))
         sorted_pool = stack.enter_context(tc.tile_pool(name="sorted", bufs=2))
         grouped_pool = stack.enter_context(tc.tile_pool(name="grouped", bufs=ROUND))
-        codes_pool = stack.enter_context(tc.tile_pool(name="codes", bufs=4 * ROUND))
+        codes_pool = stack.enter_context(tc.tile_pool(name="codes", bufs=7 * ROUND))
         turn_psum = stack.enter_context(tc.psum_pool(name="turn", bufs=ROUND))
         acc_psum = stack.enter_context(tc.psum_pool(name="acc", bufs=1))
 
@@ -78,7 +78,7 @@ def tile_share_lstm_cell_pa_k_kernel(
         n_rounds = len(rounds)
         small_step = n_rounds - 3
         late_lstm = n_rounds - 2
-        late_shared = n_rounds - 3
+        late_shared = n_rounds - 5
 
         ident_f32 = keep.tile([P, P], F32, name="ident_f32")
         make_identity(nc, ident_f32[:])
@@ -113,8 +113,9 @@ def tile_share_lstm_cell_pa_k_kernel(
         nc.gpsimd.dma_start(out=c_rows[:], in_=c_minors.rearrange("(rt p) d -> p rt d", p=P))
 
         words_view = weight_ih_words.bitcast(I32)
-        scales_view = weight_ih_scales.bitcast(I32).rearrange("g (h q) n -> q h g n", h=2)
+        scales_view = weight_ih_scales.bitcast(I32).rearrange("g (q r) n -> r q g n", r=4)
         w_planes = {}
+        plane_of = {}
         w_words = {}
         x_rows = {}
         x_words = {}
@@ -124,29 +125,34 @@ def tile_share_lstm_cell_pa_k_kernel(
         def load_x(r):
             first, size = rounds[r]
             x_rows[r] = x_pool.tile([P, ROW_TILES, size * K_PASS], BF16, name="x_rows")
-            for rt in range(ROW_TILES):
+            nc.sync.dma_start(
+                out=x_rows[r][:],
+                in_=x[:, first * K_PASS : (first + size) * K_PASS].rearrange("(rt p) k -> p rt k", p=P),
+            )
+
+        def zero_planes(first):
+            w_planes[first] = keep.tile([P, SCALE_GROUP, GATES], U8, name="w_planes%d" % first, align_bytes=64)
+            nc.vector.memset(w_planes[first][:].bitcast(I32), 0)
+            for i in range(SCALE_GROUP):
+                plane_of[first + i] = w_planes[first][:, i, :]
+
+        def load_scales(first):
+            for row in range(4):
                 nc.sync.dma_start(
-                    out=x_rows[r][:, rt, :], in_=x[rt * P : (rt + 1) * P, first * K_PASS : (first + size) * K_PASS]
+                    out=w_planes[first][row:P:32, :, :].bitcast(I32),
+                    in_=scales_view[row, :, first : first + SCALE_GROUP, :],
                 )
 
         def load_w(r):
             first, size = rounds[r]
-            if first % SCALE_GROUP == 0:
-                group = first // SCALE_GROUP
-                planes = keep.tile([P, SCALE_GROUP, GATES], U8, name="w_planes%d" % group, align_bytes=64)
-                nc.vector.memset(planes[:].bitcast(I32), 0)
-                for q in range(8):
-                    partition = 32 * (q // 4) + q % 4
-                    nc.sync.dma_start(
-                        out=planes[partition:P:64, :, :].bitcast(I32),
-                        in_=scales_view[q, :, first : first + SCALE_GROUP, :],
-                    )
-                w_planes[group] = planes
             w_words[r] = keep.tile([P, size, 2 * GATES], U8, name="w_words%d" % r, align_bytes=64)
             nc.sync.dma_start(
                 out=w_words[r][:].bitcast(I32),
                 in_=words_view[first : first + size].rearrange("g p n -> p g n"),
             )
+            following = first + size
+            if following % SCALE_GROUP == 0 and following < PASSES:
+                load_scales(following)
 
         def sort_round(r):
             size = rounds[r][1]
@@ -193,7 +199,7 @@ def tile_share_lstm_cell_pa_k_kernel(
                         lhsT=x_codes[g][:, rt * P : (rt + 1) * P].bitcast(FP8X4),
                         lhsT_scale=x_planes[g][:, rt * P : (rt + 1) * P],
                         rhs=w_words[r][:, i, 2 * column : 2 * (column + width)].bitcast(FP4X4),
-                        rhs_scale=w_planes[g // SCALE_GROUP][:, g % SCALE_GROUP, column : column + width],
+                        rhs_scale=plane_of[g][:, column : column + width],
                         start=(r == first_round and i == 0 and n == 0),
                         stop=(r == last_round and i == size - 1 and n == len(pieces) - 1),
                     )
@@ -236,7 +242,10 @@ def tile_share_lstm_cell_pa_k_kernel(
                     )
                 nc.vector.tensor_copy(out=plain[:, rt, LSTM_GATES:GATES], in_=share_bank[:])
 
+        zero_planes(0)
+        zero_planes(ROUND)
         load_x(0)
+        load_scales(0)
         for r in range(1, X_AHEAD):
             load_x(r)
             load_w(r - 1)
@@ -244,6 +253,7 @@ def tile_share_lstm_cell_pa_k_kernel(
             if step < n_rounds:
                 sort_round(step)
             if step + X_AHEAD < n_rounds:
+                zero_planes(rounds[step + X_AHEAD][0])
                 load_x(step + X_AHEAD)
             if step + X_AHEAD - 1 < n_rounds:
                 load_w(step + X_AHEAD - 1)
@@ -262,10 +272,8 @@ def tile_share_lstm_cell_pa_k_kernel(
                     multiply(acc[1][rt], rt, WINDOWS[1], r, 0, late_shared - 1)
 
         both = range(ROW_TILES)
-        pre = keep.tile([P, ROW_TILES, LSTM_GATES], F32, name="pre")
         gate = keep.tile([P, ROW_TILES, LSTM_GATES], F32, name="gate")
         base = keep.tile([P, ROW_TILES, 3 * D_H], F32, name="base")
-        pre_b = [[keep.tile([P, D_H], F32, name="pre_b%d%d" % (j, rt)) for rt in both] for j in range(3)]
         share = [[keep.tile([P, D_H], F32, name="share%d%d" % (j, rt)) for rt in both] for j in range(3)]
         kept = [keep.tile([P, D_H], F32, name="kept%d" % rt) for rt in both]
         fresh = [keep.tile([P, D_H], F32, name="fresh%d" % rt) for rt in both]
@@ -286,9 +294,9 @@ def tile_share_lstm_cell_pa_k_kernel(
             nc.sync.dma_start(out=out.rearrange("(rt p) d -> p rt d", p=P), in_=result[:])
 
         def gates(rt):
-            nc.vector.tensor_tensor(out=pre[:, rt, :], in0=acc[0][rt][:], in1=plain[:, rt, 0:LSTM_GATES], op=ALU.add)
-            nc.scalar.activation(out=gate[:, rt, 0 : 3 * D_H], in_=pre[:, rt, 0 : 3 * D_H], func=ACT.Sigmoid)
-            nc.scalar.activation(out=candidate[rt], in_=pre[:, rt, 3 * D_H : LSTM_GATES], func=ACT.Tanh)
+            nc.vector.tensor_tensor(out=gate[:, rt, :], in0=acc[0][rt][:], in1=plain[:, rt, 0:LSTM_GATES], op=ALU.add)
+            nc.scalar.activation(out=gate[:, rt, 0 : 3 * D_H], in_=gate[:, rt, 0 : 3 * D_H], func=ACT.Sigmoid)
+            nc.scalar.activation(out=candidate[rt], in_=candidate[rt], func=ACT.Tanh)
 
         def cell(rt):
             nc.vector.scalar_tensor_tensor(
@@ -317,11 +325,11 @@ def tile_share_lstm_cell_pa_k_kernel(
 
         def shared_gate(j, rt, bank):
             nc.vector.tensor_tensor(
-                out=pre_b[j][rt][:], in0=bank[:, 0:D_H], in1=base[:, rt, j * D_H : (j + 1) * D_H], op=ALU.add
+                out=share[j][rt][:], in0=bank[:, 0:D_H], in1=base[:, rt, j * D_H : (j + 1) * D_H], op=ALU.add
             )
-            nc.scalar.activation(out=share[j][rt][:], in_=pre_b[j][rt][:], func=ACT.Sigmoid)
+            nc.scalar.activation(out=share[j][rt][:], in_=share[j][rt][:], func=ACT.Sigmoid)
 
-        def state(j, rt):
+        def rest_of(j, rt):
             if j == 0:
                 subtracted = out_gate[rt]
             else:
@@ -334,6 +342,8 @@ def tile_share_lstm_cell_pa_k_kernel(
                 op0=ALU.add,
                 op1=ALU.subtract,
             )
+
+        def state(j, rt):
             nc.vector.scalar_tensor_tensor(
                 out=s_t[j][:, rt, :],
                 in0=rest[j][rt][:],
@@ -366,24 +376,30 @@ def tile_share_lstm_cell_pa_k_kernel(
         shared_gate(0, 0, late[0][0])
         cell(1)
         store(c_t, out_1)
+        rest_of(0, 0)
         shared_gate(0, 1, late[0][1])
         state(0, 0)
         hidden(1)
         store(h_t, out_0)
+        rest_of(0, 1)
         take_1(0)
         state(0, 1)
         store(s_t[0], out_2)
         shared_gate(1, 0, late[1][0])
         take_1(1)
-        state(1, 0)
+        rest_of(1, 0)
         shared_gate(1, 1, late[1][1])
+        state(1, 0)
+        rest_of(1, 1)
         take_2(0)
         state(1, 1)
         store(s_t[1], out_3)
         shared_gate(2, 0, late[2][0])
         take_2(1)
+        rest_of(2, 0)
+        shared_gate(2, 1, late[2][1])
         state(2, 0)
         nc.sync.dma_start(out=out_4[0:P, :], in_=s_t[2][:, 0, :])
-        shared_gate(2, 1, late[2][1])
+        rest_of(2, 1)
         state(2, 1)
         nc.sync.dma_start(out=out_4[P:BATCH, :], in_=s_t[2][:, 1, :])

@@ -65,7 +65,7 @@ def tile_share_lstm_cell_pa_k_kernel(
         x_pool = stack.enter_context(tc.tile_pool(name="x_rows", bufs=X_AHEAD))
         sorted_pool = stack.enter_context(tc.tile_pool(name="sorted", bufs=2))
         grouped_pool = stack.enter_context(tc.tile_pool(name="grouped", bufs=ROUND))
-        codes_pool = stack.enter_context(tc.tile_pool(name="codes", bufs=7 * ROUND))
+        codes_pool = stack.enter_context(tc.tile_pool(name="codes", bufs=6 * ROUND))
         turn_psum = stack.enter_context(tc.psum_pool(name="turn", bufs=ROUND))
         acc_psum = stack.enter_context(tc.psum_pool(name="acc", bufs=1))
 
@@ -78,7 +78,7 @@ def tile_share_lstm_cell_pa_k_kernel(
         n_rounds = len(rounds)
         small_step = n_rounds - 3
         late_lstm = n_rounds - 2
-        late_shared = n_rounds - 5
+        late_shared = n_rounds - 4
 
         ident_f32 = keep.tile([P, P], F32, name="ident_f32")
         make_identity(nc, ident_f32[:])
@@ -143,13 +143,22 @@ def tile_share_lstm_cell_pa_k_kernel(
                     in_=scales_view[row, :, first : first + SCALE_GROUP, :],
                 )
 
+        def load_columns(r, begin, end):
+            first, size = rounds[r]
+            words = keep.tile([P, size, 2 * (end - begin)], U8, name="w_words%d_%d" % (r, begin), align_bytes=64)
+            nc.sync.dma_start(
+                out=words[:].bitcast(I32),
+                in_=words_view[first : first + size, :, begin // 2 : end // 2].rearrange("g p n -> p g n"),
+            )
+            for column in range(begin, end, D_H):
+                w_words[r, column] = (words, begin)
+
         def load_w(r):
             first, size = rounds[r]
-            w_words[r] = keep.tile([P, size, 2 * GATES], U8, name="w_words%d" % r, align_bytes=64)
-            nc.sync.dma_start(
-                out=w_words[r][:].bitcast(I32),
-                in_=words_view[first : first + size].rearrange("g p n -> p g n"),
-            )
+            if r < late_shared:
+                load_columns(r, 0, GATES)
+            else:
+                load_columns(r, 0, LSTM_GATES)
             following = first + size
             if following % SCALE_GROUP == 0 and following < PASSES:
                 load_scales(following)
@@ -193,12 +202,13 @@ def tile_share_lstm_cell_pa_k_kernel(
             for i in range(size):
                 g = first + i
                 for n, (column, width) in enumerate(pieces):
+                    words, begin = w_words[r, column]
                     in_bank = column - pieces[0][0]
                     nc.tensor.matmul_mx(
                         out=bank[:, in_bank : in_bank + width],
                         lhsT=x_codes[g][:, rt * P : (rt + 1) * P].bitcast(FP8X4),
                         lhsT_scale=x_planes[g][:, rt * P : (rt + 1) * P],
-                        rhs=w_words[r][:, i, 2 * column : 2 * (column + width)].bitcast(FP4X4),
+                        rhs=words[:, i, 2 * (column - begin) : 2 * (column - begin + width)].bitcast(FP4X4),
                         rhs_scale=plane_of[g][:, column : column + width],
                         start=(r == first_round and i == 0 and n == 0),
                         stop=(r == last_round and i == size - 1 and n == len(pieces) - 1),
@@ -257,6 +267,9 @@ def tile_share_lstm_cell_pa_k_kernel(
                 load_x(step + X_AHEAD)
             if step + X_AHEAD - 1 < n_rounds:
                 load_w(step + X_AHEAD - 1)
+            if step + X_AHEAD == n_rounds:
+                for r in range(late_shared, n_rounds):
+                    load_columns(r, LSTM_GATES, GATES)
             if step == small_step:
                 small_transposes()
             if step == small_step + 1:
@@ -314,18 +327,14 @@ def tile_share_lstm_cell_pa_k_kernel(
                 out=h_t[:, rt, :], in0=tanh_c[rt][:], scalar=m[rt], in1=out_gate[rt], op0=ALU.mult, op1=ALU.mult
             )
 
-        def shared_sum(j, rt):
+        def late_bank(j, rt):
             if j == 0:
-                bank = acc_psum.tile([P, LSTM_GATES], F32, name="late_b0", tag="acc1%d" % rt)
-            else:
-                bank = turn_psum.tile([P, LSTM_GATES], F32, name="late_b", tag="bank")
-            for r in range(late_shared, n_rounds):
-                multiply(bank, rt, WINDOWS[1][j : j + 1], r, late_shared, n_rounds - 1)
-            return bank
+                return acc_psum.tile([P, LSTM_GATES], F32, name="late_b0", tag="acc1%d" % rt)
+            return turn_psum.tile([P, LSTM_GATES], F32, name="late_b", tag="bank")
 
-        def shared_gate(j, rt, bank):
+        def shared_gate(j, rt):
             nc.vector.tensor_tensor(
-                out=share[j][rt][:], in0=bank[:, 0:D_H], in1=base[:, rt, j * D_H : (j + 1) * D_H], op=ALU.add
+                out=share[j][rt][:], in0=late[j][rt][:, 0:D_H], in1=base[:, rt, j * D_H : (j + 1) * D_H], op=ALU.add
             )
             nc.scalar.activation(out=share[j][rt][:], in_=share[j][rt][:], func=ACT.Sigmoid)
 
@@ -355,6 +364,8 @@ def tile_share_lstm_cell_pa_k_kernel(
 
         def take_1(rt):
             nc.vector.tensor_tensor(out=taken[1][rt][:], in0=out_gate[rt], in1=s_t[0][:, rt, :], op=ALU.add)
+
+        def take_more(rt):
             nc.vector.tensor_tensor(out=taken[0][rt][:], in0=taken[1][rt][:], in1=s_t[0][:, rt, :], op=ALU.add)
 
         def take_2(rt):
@@ -367,37 +378,47 @@ def tile_share_lstm_cell_pa_k_kernel(
         for rt in both:
             for r in range(late_lstm, n_rounds):
                 multiply(acc[0][rt], rt, WINDOWS[0], r, 0, n_rounds - 1)
-        late = [[shared_sum(j, rt) for rt in both] for j in range(3)]
+        late = [[late_bank(j, rt) for rt in both] for j in range(3)]
+        for r in range(late_shared, late_lstm):
+            for rt in both:
+                for j in range(3):
+                    multiply(late[j][rt], rt, WINDOWS[1][j : j + 1], r, late_shared, n_rounds - 1)
+        for j in range(3):
+            for rt in both:
+                for r in range(late_lstm, n_rounds):
+                    multiply(late[j][rt], rt, WINDOWS[1][j : j + 1], r, late_shared, n_rounds - 1)
 
         gates(0)
         cell(0)
         gates(1)
         hidden(0)
-        shared_gate(0, 0, late[0][0])
         cell(1)
         store(c_t, out_1)
-        rest_of(0, 0)
-        shared_gate(0, 1, late[0][1])
-        state(0, 0)
         hidden(1)
         store(h_t, out_0)
+        shared_gate(0, 0)
+        shared_gate(0, 1)
+        rest_of(0, 0)
         rest_of(0, 1)
-        take_1(0)
+        state(0, 0)
         state(0, 1)
         store(s_t[0], out_2)
-        shared_gate(1, 0, late[1][0])
+        shared_gate(1, 0)
+        take_1(0)
         take_1(1)
+        shared_gate(1, 1)
+        take_more(0)
         rest_of(1, 0)
-        shared_gate(1, 1, late[1][1])
-        state(1, 0)
+        take_more(1)
         rest_of(1, 1)
-        take_2(0)
+        state(1, 0)
         state(1, 1)
         store(s_t[1], out_3)
-        shared_gate(2, 0, late[2][0])
+        shared_gate(2, 0)
+        take_2(0)
         take_2(1)
         rest_of(2, 0)
-        shared_gate(2, 1, late[2][1])
+        shared_gate(2, 1)
         state(2, 0)
         nc.sync.dma_start(out=out_4[0:P, :], in_=s_t[2][:, 0, :])
         rest_of(2, 1)

@@ -27,6 +27,7 @@ WINDOWS = (
 
 ROUND = 4
 X_AHEAD = 4
+SMALL_AT = 1
 SCALE_GROUP = ROUND
 
 FLOPS = 2 * BATCH * D_IN * GATES + 2 * BATCH * D_H * GATES
@@ -76,10 +77,20 @@ def tile_share_lstm_cell_pa_k_kernel(
             rounds.append((first_pass, size))
             first_pass += size
         n_rounds = len(rounds)
-        small_step = n_rounds - 3
+        small_step = n_rounds - 2
         late_lstm = n_rounds - 2
         late_shared = n_rounds - 4
 
+        w_planes = {}
+        plane_of = {}
+
+        def zero_planes(first):
+            w_planes[first] = keep.tile([P, SCALE_GROUP, GATES], U8, name="w_planes%d" % first, align_bytes=64)
+            nc.vector.memset(w_planes[first][:].bitcast(I32), 0)
+            for i in range(SCALE_GROUP):
+                plane_of[first + i] = w_planes[first][:, i, :]
+
+        zero_planes(0)
         ident_f32 = keep.tile([P, P], F32, name="ident_f32")
         make_identity(nc, ident_f32[:])
         ident_bf16 = keep.tile([P, P], BF16, name="ident_bf16")
@@ -97,25 +108,22 @@ def tile_share_lstm_cell_pa_k_kernel(
         nc.scalar.activation(out=table_out[:], in_=table_in[:], func=ACT.Sigmoid)
 
         acts = keep.tile([P, 4, ROW_TILES, D_H], BF16, name="acts")
-        for j, rows in enumerate((h_minors, s0, s1, s2)):
-            nc.gpsimd.dma_start(out=acts[:, j], in_=rows.rearrange("(rt p) d -> p rt d", p=P))
         small_w = keep.tile([P, 7, D_H], BF16, name="small_w")
-        nc.gpsimd.dma_start(out=small_w[:, 0:4, :], in_=weight_hh.rearrange("(j p) d -> p j d", p=P))
+        c_rows = keep.tile([P, ROW_TILES, D_H], BF16, name="c_rows")
+        small_loads = [(acts[:, j], rows.rearrange("(rt p) d -> p rt d", p=P)) for j, rows in enumerate((h_minors, s0, s1, s2))]
+        small_loads.append((small_w[:, 0:4, :], weight_hh.rearrange("(j p) d -> p j d", p=P)))
         for j, weight in enumerate((weight_sh0, weight_sh1, weight_sh2)):
-            nc.gpsimd.dma_start(out=small_w[:, 4 + j, :], in_=weight)
+            small_loads.append((small_w[:, 4 + j, :], weight))
+        small_loads.append((c_rows[:], c_minors.rearrange("(rt p) d -> p rt d", p=P)))
         nc.gpsimd.dma_start(out=bias_rows[0:1, :], in_=bias_ih.rearrange("(o n) -> o n", o=1))
         nc.gpsimd.dma_start(out=bias_rows[1:2, 0:LSTM_GATES], in_=bias_hh.rearrange("(o n) -> o n", o=1))
         for j, bias in enumerate((bias_sh0, bias_sh1, bias_sh2)):
             first = LSTM_GATES + j * D_H
             nc.gpsimd.dma_start(out=bias_rows[1:2, first : first + D_H], in_=bias.rearrange("(o n) -> o n", o=1))
         nc.gpsimd.dma_start(out=mask_rows[0:ROW_TILES, :], in_=mask.rearrange("(rt p) -> rt p", p=P))
-        c_rows = keep.tile([P, ROW_TILES, D_H], BF16, name="c_rows")
-        nc.gpsimd.dma_start(out=c_rows[:], in_=c_minors.rearrange("(rt p) d -> p rt d", p=P))
 
         words_view = weight_ih_words.bitcast(I32)
         scales_view = weight_ih_scales.bitcast(I32).rearrange("g (q r) n -> r q g n", r=4)
-        w_planes = {}
-        plane_of = {}
         w_words = {}
         x_rows = {}
         x_words = {}
@@ -129,12 +137,6 @@ def tile_share_lstm_cell_pa_k_kernel(
                 out=x_rows[r][:],
                 in_=x[:, first * K_PASS : (first + size) * K_PASS].rearrange("(rt p) k -> p rt k", p=P),
             )
-
-        def zero_planes(first):
-            w_planes[first] = keep.tile([P, SCALE_GROUP, GATES], U8, name="w_planes%d" % first, align_bytes=64)
-            nc.vector.memset(w_planes[first][:].bitcast(I32), 0)
-            for i in range(SCALE_GROUP):
-                plane_of[first + i] = w_planes[first][:, i, :]
 
         def load_scales(first):
             for row in range(4):
@@ -224,7 +226,7 @@ def tile_share_lstm_cell_pa_k_kernel(
             for j in range(4):
                 for rt in range(ROW_TILES):
                     nc.tensor.transpose(acts_bank[:, j, rt, :], acts[:, j, rt, :], ident_bf16[:])
-            nc.vector.tensor_copy(out=acts_t[:], in_=acts_bank[:])
+            nc.scalar.copy(out=acts_t[:], in_=acts_bank[:])
             w_bank = turn_psum.tile([P, 8, P], BF16, name="w_bank", tag="bank")
             for j in range(7):
                 nc.tensor.transpose(w_bank[:, j, :], small_w[:, j, :], ident_bf16[:])
@@ -252,11 +254,12 @@ def tile_share_lstm_cell_pa_k_kernel(
                     )
                 nc.vector.tensor_copy(out=plain[:, rt, LSTM_GATES:GATES], in_=share_bank[:])
 
-        zero_planes(0)
         zero_planes(ROUND)
         load_x(0)
+        load_x(1)
+        load_columns(0, 0, GATES)
         load_scales(0)
-        for r in range(1, X_AHEAD):
+        for r in range(2, X_AHEAD):
             load_x(r)
             load_w(r - 1)
         for step in range(n_rounds + 1):
@@ -270,12 +273,15 @@ def tile_share_lstm_cell_pa_k_kernel(
             if step + X_AHEAD == n_rounds:
                 for r in range(late_shared, n_rounds):
                     load_columns(r, LSTM_GATES, GATES)
+            if SMALL_AT <= step < SMALL_AT + 3:
+                for out, in_ in small_loads[3 * (step - SMALL_AT) : 3 * (step - SMALL_AT) + 3]:
+                    nc.sync.dma_start(out=out, in_=in_)
+            if step >= 1:
+                turn_and_quantise(step - 1)
             if step == small_step:
                 small_transposes()
             if step == small_step + 1:
                 small_products()
-            if step >= 1:
-                turn_and_quantise(step - 1)
             r = step - 2
             if 0 <= r < late_lstm:
                 for rt in range(ROW_TILES):

@@ -27,7 +27,6 @@ WINDOWS = (
 
 ROUND = 4
 X_AHEAD = 4
-SMALL_AT = 1
 SCALE_GROUP = ROUND
 
 FLOPS = 2 * BATCH * D_IN * GATES + 2 * BATCH * D_H * GATES
@@ -110,11 +109,12 @@ def tile_share_lstm_cell_pa_k_kernel(
         acts = keep.tile([P, 4, ROW_TILES, D_H], BF16, name="acts")
         small_w = keep.tile([P, 7, D_H], BF16, name="small_w")
         c_rows = keep.tile([P, ROW_TILES, D_H], BF16, name="c_rows")
-        small_loads = [(acts[:, j], rows.rearrange("(rt p) d -> p rt d", p=P)) for j, rows in enumerate((h_minors, s0, s1, s2))]
-        small_loads.append((small_w[:, 0:4, :], weight_hh.rearrange("(j p) d -> p j d", p=P)))
+        for j, rows in enumerate((h_minors, s0, s1, s2)):
+            nc.gpsimd.dma_start(out=acts[:, j], in_=rows.rearrange("(rt p) d -> p rt d", p=P))
+        nc.gpsimd.dma_start(out=small_w[:, 0:4, :], in_=weight_hh.rearrange("(j p) d -> p j d", p=P))
         for j, weight in enumerate((weight_sh0, weight_sh1, weight_sh2)):
-            small_loads.append((small_w[:, 4 + j, :], weight))
-        small_loads.append((c_rows[:], c_minors.rearrange("(rt p) d -> p rt d", p=P)))
+            nc.gpsimd.dma_start(out=small_w[:, 4 + j, :], in_=weight)
+        nc.gpsimd.dma_start(out=c_rows[:], in_=c_minors.rearrange("(rt p) d -> p rt d", p=P))
         nc.gpsimd.dma_start(out=bias_rows[0:1, :], in_=bias_ih.rearrange("(o n) -> o n", o=1))
         nc.gpsimd.dma_start(out=bias_rows[1:2, 0:LSTM_GATES], in_=bias_hh.rearrange("(o n) -> o n", o=1))
         for j, bias in enumerate((bias_sh0, bias_sh1, bias_sh2)):
@@ -273,9 +273,6 @@ def tile_share_lstm_cell_pa_k_kernel(
             if step + X_AHEAD == n_rounds:
                 for r in range(late_shared, n_rounds):
                     load_columns(r, LSTM_GATES, GATES)
-            if SMALL_AT <= step < SMALL_AT + 3:
-                for out, in_ in small_loads[3 * (step - SMALL_AT) : 3 * (step - SMALL_AT) + 3]:
-                    nc.sync.dma_start(out=out, in_=in_)
             if step >= 1:
                 turn_and_quantise(step - 1)
             if step == small_step:

@@ -78,13 +78,14 @@ def tile_share_lstm_cell_pa_k_kernel(
         n_rounds = len(rounds)
         small_step = n_rounds - 2
         late_lstm = n_rounds - 2
+        by_gate = n_rounds - 3
         late_shared = n_rounds - 4
 
         w_planes = {}
         plane_of = {}
 
         def zero_planes(first):
-            w_planes[first] = keep.tile([P, SCALE_GROUP, GATES], U8, name="w_planes%d" % first, align_bytes=64)
+            w_planes[first] = keep.tile([P, SCALE_GROUP, GATES], U8, name="w_planes%d" % first, align_bytes=256)
             nc.vector.memset(w_planes[first][:].bitcast(I32), 0)
             for i in range(SCALE_GROUP):
                 plane_of[first + i] = w_planes[first][:, i, :]
@@ -109,18 +110,18 @@ def tile_share_lstm_cell_pa_k_kernel(
         acts = keep.tile([P, 4, ROW_TILES, D_H], BF16, name="acts")
         small_w = keep.tile([P, 7, D_H], BF16, name="small_w")
         c_rows = keep.tile([P, ROW_TILES, D_H], BF16, name="c_rows")
-        for j, rows in enumerate((h_minors, s0, s1, s2)):
-            nc.gpsimd.dma_start(out=acts[:, j], in_=rows.rearrange("(rt p) d -> p rt d", p=P))
-        nc.gpsimd.dma_start(out=small_w[:, 0:4, :], in_=weight_hh.rearrange("(j p) d -> p j d", p=P))
-        for j, weight in enumerate((weight_sh0, weight_sh1, weight_sh2)):
-            nc.gpsimd.dma_start(out=small_w[:, 4 + j, :], in_=weight)
-        nc.gpsimd.dma_start(out=c_rows[:], in_=c_minors.rearrange("(rt p) d -> p rt d", p=P))
         nc.gpsimd.dma_start(out=bias_rows[0:1, :], in_=bias_ih.rearrange("(o n) -> o n", o=1))
         nc.gpsimd.dma_start(out=bias_rows[1:2, 0:LSTM_GATES], in_=bias_hh.rearrange("(o n) -> o n", o=1))
         for j, bias in enumerate((bias_sh0, bias_sh1, bias_sh2)):
             first = LSTM_GATES + j * D_H
             nc.gpsimd.dma_start(out=bias_rows[1:2, first : first + D_H], in_=bias.rearrange("(o n) -> o n", o=1))
         nc.gpsimd.dma_start(out=mask_rows[0:ROW_TILES, :], in_=mask.rearrange("(rt p) -> rt p", p=P))
+        for j, rows in enumerate((h_minors, s0, s1, s2)):
+            nc.gpsimd.dma_start(out=acts[:, j], in_=rows.rearrange("(rt p) d -> p rt d", p=P))
+        nc.gpsimd.dma_start(out=small_w[:, 0:4, :], in_=weight_hh.rearrange("(j p) d -> p j d", p=P))
+        for j, weight in enumerate((weight_sh0, weight_sh1, weight_sh2)):
+            nc.gpsimd.dma_start(out=small_w[:, 4 + j, :], in_=weight)
+        nc.gpsimd.dma_start(out=c_rows[:], in_=c_minors.rearrange("(rt p) d -> p rt d", p=P))
 
         words_view = weight_ih_words.bitcast(I32)
         scales_view = weight_ih_scales.bitcast(I32).rearrange("g (q r) n -> r q g n", r=4)
@@ -132,11 +133,17 @@ def tile_share_lstm_cell_pa_k_kernel(
 
         def load_x(r):
             first, size = rounds[r]
-            x_rows[r] = x_pool.tile([P, ROW_TILES, size * K_PASS], BF16, name="x_rows")
-            nc.sync.dma_start(
-                out=x_rows[r][:],
-                in_=x[:, first * K_PASS : (first + size) * K_PASS].rearrange("(rt p) k -> p rt k", p=P),
-            )
+            columns = slice(first * K_PASS, (first + size) * K_PASS)
+            if r == 0:
+                x_rows[r] = []
+                for rt in range(ROW_TILES):
+                    first_rows = keep.tile([P, size * K_PASS], BF16, name="first_rows%d" % rt)
+                    nc.sync.dma_start(out=first_rows[:], in_=x[rt * P : (rt + 1) * P, columns])
+                    x_rows[r].append(first_rows[:])
+            else:
+                rows = x_pool.tile([P, ROW_TILES, size * K_PASS], BF16, name="x_rows")
+                nc.sync.dma_start(out=rows[:], in_=x[:, columns].rearrange("(rt p) k -> p rt k", p=P))
+                x_rows[r] = [rows[:, rt, :] for rt in range(ROW_TILES)]
 
         def load_scales(first):
             for row in range(4):
@@ -147,7 +154,7 @@ def tile_share_lstm_cell_pa_k_kernel(
 
         def load_columns(r, begin, end):
             first, size = rounds[r]
-            words = keep.tile([P, size, 2 * (end - begin)], U8, name="w_words%d_%d" % (r, begin), align_bytes=64)
+            words = keep.tile([P, size, 2 * (end - begin)], U8, name="w_words%d_%d" % (r, begin), align_bytes=256)
             nc.sync.dma_start(
                 out=words[:].bitcast(I32),
                 in_=words_view[first : first + size, :, begin // 2 : end // 2].rearrange("g p n -> p g n"),
@@ -171,25 +178,33 @@ def tile_share_lstm_cell_pa_k_kernel(
             for rt in range(ROW_TILES):
                 nc.vector.tensor_copy(
                     out=x_words[r][:, rt],
-                    in_=x_rows[r][:, rt, :].bitcast(F32).rearrange("p (g w u) -> p g u w", g=size, u=2),
+                    in_=x_rows[r][rt].bitcast(F32).rearrange("p (g w u) -> p g u w", g=size, u=2),
                 )
 
         def turn_and_quantise(r):
             first, size = rounds[r]
             for i in range(size):
-                turned = turn_psum.tile([P, ROW_TILES, 2, P], F32, name="turned", tag="bank")
-                for rt in range(ROW_TILES):
-                    for u in range(2):
-                        nc.tensor.transpose(turned[:, rt, u, :], x_words[r][:, rt, i, u, :], ident_f32[:])
-                grouped = grouped_pool.tile([P, 4 * BATCH], BF16, name="grouped", align_bytes=64)
-                nc.scalar.copy(
-                    out=grouped[:].bitcast(F32).rearrange("p (rt row u) -> p rt row u", rt=ROW_TILES, u=2),
-                    in_=turned[:].rearrange("p rt u row -> p rt row u"),
-                )
                 g = first + i
-                x_codes[g] = codes_pool.tile([P, BATCH], U32, name="x_codes", align_bytes=64)
-                x_planes[g] = codes_pool.tile([P, BATCH], U8, name="x_planes", align_bytes=64)
-                nc.vector.quantize_mx(out=x_codes[g][:].bitcast(FP8X4), scales=x_planes[g][:], in_=grouped[:])
+                turned = turn_psum.tile([P, ROW_TILES, 2, P], F32, name="turned", tag="bank")
+                grouped = grouped_pool.tile([P, 4 * BATCH], BF16, name="grouped", align_bytes=256)
+                x_codes[g] = codes_pool.tile([P, BATCH], U32, name="x_codes", align_bytes=256)
+                x_planes[g] = codes_pool.tile([P, BATCH], U8, name="x_planes", align_bytes=256)
+                step = 1 if r == 0 else ROW_TILES
+                for begin in range(0, ROW_TILES, step):
+                    end = begin + step
+                    for rt in range(begin, end):
+                        for u in range(2):
+                            nc.tensor.transpose(turned[:, rt, u, :], x_words[r][:, rt, i, u, :], ident_f32[:])
+                    values = grouped[:, 4 * P * begin : 4 * P * end]
+                    nc.scalar.copy(
+                        out=values.bitcast(F32).rearrange("p (rt row u) -> p rt row u", rt=step, u=2),
+                        in_=turned[:, begin:end].rearrange("p rt u row -> p rt row u"),
+                    )
+                    nc.vector.quantize_mx(
+                        out=x_codes[g][:, P * begin : P * end].bitcast(FP8X4),
+                        scales=x_planes[g][:, P * begin : P * end],
+                        in_=values,
+                    )
 
         acc = [
             [
@@ -199,9 +214,9 @@ def tile_share_lstm_cell_pa_k_kernel(
             for window in range(2)
         ]
 
-        def multiply(bank, rt, pieces, r, first_round, last_round):
+        def multiply(bank, rt, pieces, r, first_round, last_round, which=None):
             first, size = rounds[r]
-            for i in range(size):
+            for i in which or range(size):
                 g = first + i
                 for n, (column, width) in enumerate(pieces):
                     words, begin = w_words[r, column]
@@ -254,15 +269,27 @@ def tile_share_lstm_cell_pa_k_kernel(
                     )
                 nc.vector.tensor_copy(out=plain[:, rt, LSTM_GATES:GATES], in_=share_bank[:])
 
+        def multiply_round(r):
+            if 0 <= r < late_lstm:
+                for rt in range(ROW_TILES):
+                    multiply(acc[0][rt], rt, WINDOWS[0], r, 0, n_rounds - 1)
+            if 0 <= r < late_shared:
+                for rt in range(ROW_TILES):
+                    multiply(acc[1][rt], rt, WINDOWS[1], r, 0, late_shared - 1)
+
         zero_planes(ROUND)
         load_x(0)
-        load_x(1)
-        load_columns(0, 0, GATES)
         load_scales(0)
+        load_columns(0, 0, GATES)
+        load_x(1)
         for r in range(2, X_AHEAD):
             load_x(r)
             load_w(r - 1)
         for step in range(n_rounds + 1):
+            if 1 <= step <= 2:
+                if step - 2 >= 0 and step - 2 < 1:
+                    multiply_round(step - 2)
+                turn_and_quantise(step - 1)
             if step < n_rounds:
                 sort_round(step)
             if step + X_AHEAD < n_rounds:
@@ -273,19 +300,14 @@ def tile_share_lstm_cell_pa_k_kernel(
             if step + X_AHEAD == n_rounds:
                 for r in range(late_shared, n_rounds):
                     load_columns(r, LSTM_GATES, GATES)
-            if step >= 1:
+            if step > 2:
                 turn_and_quantise(step - 1)
             if step == small_step:
                 small_transposes()
             if step == small_step + 1:
                 small_products()
-            r = step - 2
-            if 0 <= r < late_lstm:
-                for rt in range(ROW_TILES):
-                    multiply(acc[0][rt], rt, WINDOWS[0], r, 0, n_rounds - 1)
-            if 0 <= r < late_shared:
-                for rt in range(ROW_TILES):
-                    multiply(acc[1][rt], rt, WINDOWS[1], r, 0, late_shared - 1)
+            if 1 <= step - 2:
+                multiply_round(step - 2)
 
         both = range(ROW_TILES)
         gate = keep.tile([P, ROW_TILES, LSTM_GATES], F32, name="gate")
@@ -382,14 +404,16 @@ def tile_share_lstm_cell_pa_k_kernel(
             for r in range(late_lstm, n_rounds):
                 multiply(acc[0][rt], rt, WINDOWS[0], r, 0, n_rounds - 1)
         late = [[late_bank(j, rt) for rt in both] for j in range(3)]
-        for r in range(late_shared, late_lstm):
-            for rt in both:
-                for j in range(3):
-                    multiply(late[j][rt], rt, WINDOWS[1][j : j + 1], r, late_shared, n_rounds - 1)
+        for r in range(late_shared, by_gate):
+            for i in range(rounds[r][1]):
+                for rt in both:
+                    for j in range(3):
+                        multiply(late[j][rt], rt, WINDOWS[1][j : j + 1], r, late_shared, n_rounds - 1, (i,))
         for j in range(3):
-            for rt in both:
-                for r in range(late_lstm, n_rounds):
-                    multiply(late[j][rt], rt, WINDOWS[1][j : j + 1], r, late_shared, n_rounds - 1)
+            for r in range(by_gate, n_rounds):
+                for i in range(rounds[r][1]):
+                    for rt in both:
+                        multiply(late[j][rt], rt, WINDOWS[1][j : j + 1], r, late_shared, n_rounds - 1, (i,))
 
         gates(0)
         cell(0)
@@ -417,13 +441,12 @@ def tile_share_lstm_cell_pa_k_kernel(
         state(1, 0)
         state(1, 1)
         store(s_t[1], out_3)
-        shared_gate(2, 0)
         take_2(0)
         take_2(1)
-        rest_of(2, 0)
+        shared_gate(2, 0)
         shared_gate(2, 1)
-        state(2, 0)
-        nc.sync.dma_start(out=out_4[0:P, :], in_=s_t[2][:, 0, :])
+        rest_of(2, 0)
         rest_of(2, 1)
+        state(2, 0)
         state(2, 1)
-        nc.sync.dma_start(out=out_4[P:BATCH, :], in_=s_t[2][:, 1, :])
+        store(s_t[2], out_4)

@@ -27,6 +27,7 @@ WINDOWS = (
 
 ROUND = 4
 X_AHEAD = 4
+PLANE_PITCH = 2 * LSTM_GATES
 SCALE_GROUP = ROUND
 
 FLOPS = 2 * BATCH * D_IN * GATES + 2 * BATCH * D_H * GATES
@@ -85,10 +86,11 @@ def tile_share_lstm_cell_pa_k_kernel(
         plane_of = {}
 
         def zero_planes(first):
-            w_planes[first] = keep.tile([P, SCALE_GROUP, GATES], U8, name="w_planes%d" % first, align_bytes=256)
-            nc.vector.memset(w_planes[first][:].bitcast(I32), 0)
+            tile = keep.tile([P, SCALE_GROUP, PLANE_PITCH], U8, name="w_planes%d" % first, align_bytes=256)
+            w_planes[first] = tile[:, :, 0:GATES]
+            nc.vector.memset(w_planes[first].bitcast(I32), 0)
             for i in range(SCALE_GROUP):
-                plane_of[first + i] = w_planes[first][:, i, :]
+                plane_of[first + i] = tile[:, i, 0:GATES]
 
         zero_planes(0)
         ident_f32 = keep.tile([P, P], F32, name="ident_f32")
@@ -164,13 +166,12 @@ def tile_share_lstm_cell_pa_k_kernel(
 
         def load_w(r):
             first, size = rounds[r]
+            if first > 0 and first % SCALE_GROUP == 0:
+                load_scales(first)
             if r < late_shared:
                 load_columns(r, 0, GATES)
             else:
                 load_columns(r, 0, LSTM_GATES)
-            following = first + size
-            if following % SCALE_GROUP == 0 and following < PASSES:
-                load_scales(following)
 
         def sort_round(r):
             size = rounds[r][1]
@@ -185,20 +186,20 @@ def tile_share_lstm_cell_pa_k_kernel(
             first, size = rounds[r]
             for i in range(size):
                 g = first + i
-                turned = turn_psum.tile([P, ROW_TILES, 2, P], F32, name="turned", tag="bank")
                 grouped = grouped_pool.tile([P, 4 * BATCH], BF16, name="grouped", align_bytes=256)
                 x_codes[g] = codes_pool.tile([P, BATCH], U32, name="x_codes", align_bytes=256)
                 x_planes[g] = codes_pool.tile([P, BATCH], U8, name="x_planes", align_bytes=256)
-                step = 1 if r == 0 else ROW_TILES
-                for begin in range(0, ROW_TILES, step):
-                    end = begin + step
+                tiles = 1 if r == 0 else ROW_TILES
+                for begin in range(0, ROW_TILES, tiles):
+                    end = begin + tiles
+                    turned = turn_psum.tile([P, tiles, 2, P], F32, name="turned", tag="bank")
                     for rt in range(begin, end):
                         for u in range(2):
-                            nc.tensor.transpose(turned[:, rt, u, :], x_words[r][:, rt, i, u, :], ident_f32[:])
+                            nc.tensor.transpose(turned[:, rt - begin, u, :], x_words[r][:, rt, i, u, :], ident_f32[:])
                     values = grouped[:, 4 * P * begin : 4 * P * end]
                     nc.scalar.copy(
-                        out=values.bitcast(F32).rearrange("p (rt row u) -> p rt row u", rt=step, u=2),
-                        in_=turned[:, begin:end].rearrange("p rt u row -> p rt row u"),
+                        out=values.bitcast(F32).rearrange("p (rt row u) -> p rt row u", rt=tiles, u=2),
+                        in_=turned[:].rearrange("p rt u row -> p rt row u"),
                     )
                     nc.vector.quantize_mx(
                         out=x_codes[g][:, P * begin : P * end].bitcast(FP8X4),
@@ -277,7 +278,6 @@ def tile_share_lstm_cell_pa_k_kernel(
                 for rt in range(ROW_TILES):
                     multiply(acc[1][rt], rt, WINDOWS[1], r, 0, late_shared - 1)
 
-        zero_planes(ROUND)
         load_x(0)
         load_scales(0)
         load_columns(0, 0, GATES)
@@ -286,22 +286,25 @@ def tile_share_lstm_cell_pa_k_kernel(
             load_x(r)
             load_w(r - 1)
         for step in range(n_rounds + 1):
-            if 1 <= step <= 2:
-                if step - 2 >= 0 and step - 2 < 1:
-                    multiply_round(step - 2)
-                turn_and_quantise(step - 1)
+            if step == 1:
+                turn_and_quantise(0)
+            if step == 2:
+                multiply_round(0)
             if step < n_rounds:
                 sort_round(step)
+            if step == 0:
+                zero_planes(rounds[X_AHEAD - 1][0])
             if step + X_AHEAD < n_rounds:
-                zero_planes(rounds[step + X_AHEAD][0])
                 load_x(step + X_AHEAD)
             if step + X_AHEAD - 1 < n_rounds:
                 load_w(step + X_AHEAD - 1)
             if step + X_AHEAD == n_rounds:
                 for r in range(late_shared, n_rounds):
                     load_columns(r, LSTM_GATES, GATES)
-            if step > 2:
+            if step >= 2:
                 turn_and_quantise(step - 1)
+            if step + X_AHEAD < n_rounds:
+                zero_planes(rounds[step + X_AHEAD][0])
             if step == small_step:
                 small_transposes()
             if step == small_step + 1:

@@ -100,9 +100,7 @@ def tile_share_lstm_cell_pa_k_kernel(
         ones = keep.tile([P, P], BF16, name="ones")
         nc.vector.memset(ones[:], 1.0)
         bias_rows = keep.tile([P, GATES], BF16, name="bias_rows")
-        nc.vector.memset(bias_rows[:], 0.0)
         mask_rows = keep.tile([P, P], BF16, name="mask_rows")
-        nc.vector.memset(mask_rows[:], 0.0)
 
         table_in = keep.tile([P, 1], F32, name="table_in")
         nc.vector.memset(table_in[:], 0.0)
@@ -112,18 +110,22 @@ def tile_share_lstm_cell_pa_k_kernel(
         acts = keep.tile([P, 4, ROW_TILES, D_H], BF16, name="acts")
         small_w = keep.tile([P, 7, D_H], BF16, name="small_w")
         c_rows = keep.tile([P, ROW_TILES, D_H], BF16, name="c_rows")
-        nc.gpsimd.dma_start(out=bias_rows[0:1, :], in_=bias_ih.rearrange("(o n) -> o n", o=1))
-        nc.gpsimd.dma_start(out=bias_rows[1:2, 0:LSTM_GATES], in_=bias_hh.rearrange("(o n) -> o n", o=1))
-        for j, bias in enumerate((bias_sh0, bias_sh1, bias_sh2)):
-            first = LSTM_GATES + j * D_H
-            nc.gpsimd.dma_start(out=bias_rows[1:2, first : first + D_H], in_=bias.rearrange("(o n) -> o n", o=1))
-        nc.gpsimd.dma_start(out=mask_rows[0:ROW_TILES, :], in_=mask.rearrange("(rt p) -> rt p", p=P))
-        for j, rows in enumerate((h_minors, s0, s1, s2)):
-            nc.gpsimd.dma_start(out=acts[:, j], in_=rows.rearrange("(rt p) d -> p rt d", p=P))
-        nc.gpsimd.dma_start(out=small_w[:, 0:4, :], in_=weight_hh.rearrange("(j p) d -> p j d", p=P))
-        for j, weight in enumerate((weight_sh0, weight_sh1, weight_sh2)):
-            nc.gpsimd.dma_start(out=small_w[:, 4 + j, :], in_=weight)
-        nc.gpsimd.dma_start(out=c_rows[:], in_=c_minors.rearrange("(rt p) d -> p rt d", p=P))
+
+        def small_loads():
+            nc.vector.memset(bias_rows[:], 0.0)
+            nc.vector.memset(mask_rows[:], 0.0)
+            nc.gpsimd.dma_start(out=bias_rows[0:1, :], in_=bias_ih.rearrange("(o n) -> o n", o=1))
+            nc.gpsimd.dma_start(out=bias_rows[1:2, 0:LSTM_GATES], in_=bias_hh.rearrange("(o n) -> o n", o=1))
+            for j, bias in enumerate((bias_sh0, bias_sh1, bias_sh2)):
+                first = LSTM_GATES + j * D_H
+                nc.gpsimd.dma_start(out=bias_rows[1:2, first : first + D_H], in_=bias.rearrange("(o n) -> o n", o=1))
+            nc.gpsimd.dma_start(out=mask_rows[0:ROW_TILES, :], in_=mask.rearrange("(rt p) -> rt p", p=P))
+            for j, rows in enumerate((h_minors, s0, s1, s2)):
+                nc.gpsimd.dma_start(out=acts[:, j], in_=rows.rearrange("(rt p) d -> p rt d", p=P))
+            nc.gpsimd.dma_start(out=small_w[:, 0:4, :], in_=weight_hh.rearrange("(j p) d -> p j d", p=P))
+            for j, weight in enumerate((weight_sh0, weight_sh1, weight_sh2)):
+                nc.gpsimd.dma_start(out=small_w[:, 4 + j, :], in_=weight)
+            nc.gpsimd.dma_start(out=c_rows[:], in_=c_minors.rearrange("(rt p) d -> p rt d", p=P))
 
         words_view = weight_ih_words.bitcast(I32)
         scales_view = weight_ih_scales.bitcast(I32).rearrange("g (q r) n -> r q g n", r=4)
@@ -305,6 +307,8 @@ def tile_share_lstm_cell_pa_k_kernel(
                 turn_and_quantise(step - 1)
             if step + X_AHEAD < n_rounds:
                 zero_planes(rounds[step + X_AHEAD][0])
+            if step == 1:
+                small_loads()
             if step == small_step:
                 small_transposes()
             if step == small_step + 1:

from contextlib import ExitStack

import concourse.mybir as mybir
from concourse.masks import make_identity

F32 = mybir.dt.float32
BF16 = mybir.dt.bfloat16
I32 = mybir.dt.int32
U32 = mybir.dt.uint32
U8 = mybir.dt.uint8
FP8X4 = mybir.dt.float8_e4m3fn_x4
FP4X4 = mybir.dt.float4_e2m1fn_x4
ACT = mybir.ActivationFunctionType
ALU = mybir.AluOpType

P = 128
BATCH, D_IN, D_H = 256, 16384, 128
ROW_TILES = BATCH // P
GATES = 7 * D_H
LSTM_GATES = 4 * D_H
K_PASS = 4 * P
PASSES = D_IN // K_PASS
WINDOWS = (
    ((0, LSTM_GATES),),
    ((LSTM_GATES, D_H), (LSTM_GATES + D_H, D_H), (LSTM_GATES + 2 * D_H, D_H)),
)

ROUND = 4
X_AHEAD = 4
PLANE_PITCH = 2 * LSTM_GATES
SCALE_GROUP = ROUND

FLOPS = 2 * BATCH * D_IN * GATES + 2 * BATCH * D_H * GATES


def tile_share_lstm_cell_pa_k_kernel(
    tc,
    x,
    h_minors,
    c_minors,
    s0,
    s1,
    s2,
    mask,
    weight_ih_words,
    weight_ih_scales,
    bias_ih,
    weight_hh,
    bias_hh,
    weight_sh0,
    bias_sh0,
    weight_sh1,
    bias_sh1,
    weight_sh2,
    bias_sh2,
    out_0,
    out_1,
    out_2,
    out_3,
    out_4,
):
    nc = tc.nc
    with ExitStack() as stack:
        stack.enter_context(tc.manual_schedule())
        keep = stack.enter_context(tc.tile_pool(name="keep", bufs=1))
        x_pool = stack.enter_context(tc.tile_pool(name="x_rows", bufs=X_AHEAD))
        sorted_pool = stack.enter_context(tc.tile_pool(name="sorted", bufs=2))
        grouped_pool = stack.enter_context(tc.tile_pool(name="grouped", bufs=ROUND))
        codes_pool = stack.enter_context(tc.tile_pool(name="codes", bufs=6 * ROUND))
        turn_psum = stack.enter_context(tc.psum_pool(name="turn", bufs=ROUND))
        acc_psum = stack.enter_context(tc.psum_pool(name="acc", bufs=1))

        rounds = []
        first_pass = 0
        while first_pass < PASSES:
            size = min(max(first_pass, 1), ROUND)
            rounds.append((first_pass, size))
            first_pass += size
        n_rounds = len(rounds)
        small_step = n_rounds - 2
        late_lstm = n_rounds - 2
        by_gate = n_rounds - 3
        late_shared = n_rounds - 4

        w_planes = {}
        plane_of = {}

        def zero_planes(first):
            tile = keep.tile([P, SCALE_GROUP, PLANE_PITCH], U8, name="w_planes%d" % first, align_bytes=256)
            w_planes[first] = tile[:, :, 0:GATES]
            nc.vector.memset(w_planes[first].bitcast(I32), 0)
            for i in range(SCALE_GROUP):
                plane_of[first + i] = tile[:, i, 0:GATES]

        zero_planes(0)
        ident_f32 = keep.tile([P, P], F32, name="ident_f32")
        make_identity(nc, ident_f32[:])
        ident_bf16 = keep.tile([P, P], BF16, name="ident_bf16")
        make_identity(nc, ident_bf16[:])
        ones = keep.tile([P, P], BF16, name="ones")
        nc.vector.memset(ones[:], 1.0)
        bias_rows = keep.tile([P, GATES], BF16, name="bias_rows")
        mask_rows = keep.tile([P, P], BF16, name="mask_rows")

        table_in = keep.tile([P, 1], F32, name="table_in")
        nc.vector.memset(table_in[:], 0.0)
        table_out = keep.tile([P, 1], F32, name="table_out")
        nc.scalar.activation(out=table_out[:], in_=table_in[:], func=ACT.Sigmoid)

        acts = keep.tile([P, 4, ROW_TILES, D_H], BF16, name="acts")
        small_w = keep.tile([P, 7, D_H], BF16, name="small_w")
        c_rows = keep.tile([P, ROW_TILES, D_H], BF16, name="c_rows")

        def small_loads():
            nc.vector.memset(bias_rows[:], 0.0)
            nc.vector.memset(mask_rows[:], 0.0)
            nc.gpsimd.dma_start(out=bias_rows[0:1, :], in_=bias_ih.rearrange("(o n) -> o n", o=1))
            nc.gpsimd.dma_start(out=bias_rows[1:2, 0:LSTM_GATES], in_=bias_hh.rearrange("(o n) -> o n", o=1))
            for j, bias in enumerate((bias_sh0, bias_sh1, bias_sh2)):
                first = LSTM_GATES + j * D_H
                nc.gpsimd.dma_start(out=bias_rows[1:2, first : first + D_H], in_=bias.rearrange("(o n) -> o n", o=1))
            nc.gpsimd.dma_start(out=mask_rows[0:ROW_TILES, :], in_=mask.rearrange("(rt p) -> rt p", p=P))
            for j, rows in enumerate((h_minors, s0, s1, s2)):
                nc.gpsimd.dma_start(out=acts[:, j], in_=rows.rearrange("(rt p) d -> p rt d", p=P))
            nc.gpsimd.dma_start(out=small_w[:, 0:4, :], in_=weight_hh.rearrange("(j p) d -> p j d", p=P))
            for j, weight in enumerate((weight_sh0, weight_sh1, weight_sh2)):
                nc.gpsimd.dma_start(out=small_w[:, 4 + j, :], in_=weight)
            nc.gpsimd.dma_start(out=c_rows[:], in_=c_minors.rearrange("(rt p) d -> p rt d", p=P))

        words_view = weight_ih_words.bitcast(I32)
        scales_view = weight_ih_scales.bitcast(I32).rearrange("g (q r) n -> r q g n", r=4)
        w_words = {}
        x_rows = {}
        x_words = {}
        x_codes = {}
        x_planes = {}

        def load_x(r):
            first, size = rounds[r]
            columns = slice(first * K_PASS, (first + size) * K_PASS)
            if r == 0:
                x_rows[r] = []
                for rt in range(ROW_TILES):
                    first_rows = keep.tile([P, size * K_PASS], BF16, name="first_rows%d" % rt)
                    nc.sync.dma_start(out=first_rows[:], in_=x[rt * P : (rt + 1) * P, columns])
                    x_rows[r].append(first_rows[:])
            else:
                rows = x_pool.tile([P, ROW_TILES, size * K_PASS], BF16, name="x_rows")
                nc.sync.dma_start(out=rows[:], in_=x[:, columns].rearrange("(rt p) k -> p rt k", p=P))
                x_rows[r] = [rows[:, rt, :] for rt in range(ROW_TILES)]

        def load_scales(first):
            for row in range(4):
                nc.sync.dma_start(
                    out=w_planes[first][row:P:32, :, :].bitcast(I32),
                    in_=scales_view[row, :, first : first + SCALE_GROUP, :],
                )

        def load_columns(r, begin, end):
            first, size = rounds[r]
            words = keep.tile([P, size, 2 * (end - begin)], U8, name="w_words%d_%d" % (r, begin), align_bytes=256)
            nc.sync.dma_start(
                out=words[:].bitcast(I32),
                in_=words_view[first : first + size, :, begin // 2 : end // 2].rearrange("g p n -> p g n"),
            )
            for column in range(begin, end, D_H):
                w_words[r, column] = (words, begin)

        def load_w(r):
            first, size = rounds[r]
            if first > 0 and first % SCALE_GROUP == 0:
                load_scales(first)
            if r < late_shared:
                load_columns(r, 0, GATES)
            else:
                load_columns(r, 0, LSTM_GATES)

        def sort_round(r):
            size = rounds[r][1]
            x_words[r] = sorted_pool.tile([P, ROW_TILES, size, 2, P], F32, name="x_words")
            for rt in range(ROW_TILES):
                nc.vector.tensor_copy(
                    out=x_words[r][:, rt],
                    in_=x_rows[r][rt].bitcast(F32).rearrange("p (g w u) -> p g u w", g=size, u=2),
                )

        def turn_and_quantise(r):
            first, size = rounds[r]
            for i in range(size):
                g = first + i
                grouped = grouped_pool.tile([P, 4 * BATCH], BF16, name="grouped", align_bytes=256)
                x_codes[g] = codes_pool.tile([P, BATCH], U32, name="x_codes", align_bytes=256)
                x_planes[g] = codes_pool.tile([P, BATCH], U8, name="x_planes", align_bytes=256)
                tiles = 1 if r == 0 else ROW_TILES
                for begin in range(0, ROW_TILES, tiles):
                    end = begin + tiles
                    turned = turn_psum.tile([P, tiles, 2, P], F32, name="turned", tag="bank")
                    for rt in range(begin, end):
                        for u in range(2):
                            nc.tensor.transpose(turned[:, rt - begin, u, :], x_words[r][:, rt, i, u, :], ident_f32[:])
                    values = grouped[:, 4 * P * begin : 4 * P * end]
                    nc.scalar.copy(
                        out=values.bitcast(F32).rearrange("p (rt row u) -> p rt row u", rt=tiles, u=2),
                        in_=turned[:].rearrange("p rt u row -> p rt row u"),
                    )
                    nc.vector.quantize_mx(
                        out=x_codes[g][:, P * begin : P * end].bitcast(FP8X4),
                        scales=x_planes[g][:, P * begin : P * end],
                        in_=values,
                    )

        acc = [
            [
                acc_psum.tile([P, LSTM_GATES], F32, name="acc%d%d" % (window, rt), tag="acc%d%d" % (window, rt))
                for rt in range(ROW_TILES)
            ]
            for window in range(2)
        ]

        def multiply(bank, rt, pieces, r, first_round, last_round, which=None):
            first, size = rounds[r]
            for i in which or range(size):
                g = first + i
                for n, (column, width) in enumerate(pieces):
                    words, begin = w_words[r, column]
                    in_bank = column - pieces[0][0]
                    nc.tensor.matmul_mx(
                        out=bank[:, in_bank : in_bank + width],
                        lhsT=x_codes[g][:, rt * P : (rt + 1) * P].bitcast(FP8X4),
                        lhsT_scale=x_planes[g][:, rt * P : (rt + 1) * P],
                        rhs=words[:, i, 2 * (column - begin) : 2 * (column - begin + width)].bitcast(FP4X4),
                        rhs_scale=plane_of[g][:, column : column + width],
                        start=(r == first_round and i == 0 and n == 0),
                        stop=(r == last_round and i == size - 1 and n == len(pieces) - 1),
                    )

        acts_t = keep.tile([P, 4, ROW_TILES, P], BF16, name="acts_t")
        small_w_t = keep.tile([P, GATES], BF16, name="small_w_t")
        row_mask = keep.tile([P, ROW_TILES], F32, name="row_mask")
        plain = keep.tile([P, ROW_TILES, GATES], F32, name="plain")

        def small_transposes():
            acts_bank = turn_psum.tile([P, 4, ROW_TILES, P], BF16, name="acts_bank", tag="bank")
            for j in range(4):
                for rt in range(ROW_TILES):
                    nc.tensor.transpose(acts_bank[:, j, rt, :], acts[:, j, rt, :], ident_bf16[:])
            nc.scalar.copy(out=acts_t[:], in_=acts_bank[:])
            w_bank = turn_psum.tile([P, 8, P], BF16, name="w_bank", tag="bank")
            for j in range(7):
                nc.tensor.transpose(w_bank[:, j, :], small_w[:, j, :], ident_bf16[:])
            nc.tensor.transpose(w_bank[:, 7, :], mask_rows[:], ident_bf16[:])
            nc.scalar.copy(out=small_w_t[:].rearrange("p (j n) -> p j n", j=7), in_=w_bank[:, 0:7, :])
            nc.scalar.copy(out=row_mask[:], in_=w_bank[:, 7, 0:ROW_TILES])

        def small_products():
            for rt in range(ROW_TILES):
                lstm_bank = turn_psum.tile([P, LSTM_GATES], F32, name="lstm_bank", tag="bank")
                nc.tensor.matmul(
                    lstm_bank[:], lhsT=acts_t[:, 0, rt, :], rhs=small_w_t[:, 0:LSTM_GATES], start=True, stop=False
                )
                nc.tensor.matmul(lstm_bank[:], lhsT=ones[:], rhs=bias_rows[:, 0:LSTM_GATES], start=False, stop=True)
                nc.scalar.copy(out=plain[:, rt, 0:LSTM_GATES], in_=lstm_bank[:])
                share_bank = turn_psum.tile([P, 3 * D_H], F32, name="share_bank", tag="bank")
                nc.tensor.matmul(share_bank[:], lhsT=ones[:], rhs=bias_rows[:, LSTM_GATES:GATES], start=True, stop=False)
                for j in range(3):
                    nc.tensor.matmul(
                        share_bank[:, j * D_H : (j + 1) * D_H],
                        lhsT=acts_t[:, 1 + j, rt, :],
                        rhs=small_w_t[:, LSTM_GATES + j * D_H : LSTM_GATES + (j + 1) * D_H],
                        start=False,
                        stop=(j == 2),
                    )
                nc.vector.tensor_copy(out=plain[:, rt, LSTM_GATES:GATES], in_=share_bank[:])

        def multiply_round(r):
            if 0 <= r < late_lstm:
                for rt in range(ROW_TILES):
                    multiply(acc[0][rt], rt, WINDOWS[0], r, 0, n_rounds - 1)
            if 0 <= r < late_shared:
                for rt in range(ROW_TILES):
                    multiply(acc[1][rt], rt, WINDOWS[1], r, 0, late_shared - 1)

        load_x(0)
        load_scales(0)
        load_columns(0, 0, GATES)
        load_x(1)
        for r in range(2, X_AHEAD):
            load_x(r)
            load_w(r - 1)
        for step in range(n_rounds + 1):
            if step == 1:
                turn_and_quantise(0)
            if step == 2:
                multiply_round(0)
            if step < n_rounds:
                sort_round(step)
            if step == 0:
                zero_planes(rounds[X_AHEAD - 1][0])
            if step + X_AHEAD < n_rounds:
                load_x(step + X_AHEAD)
            if step + X_AHEAD - 1 < n_rounds:
                load_w(step + X_AHEAD - 1)
            if step + X_AHEAD == n_rounds:
                for r in range(late_shared, n_rounds):
                    load_columns(r, LSTM_GATES, GATES)
            if step >= 2:
                turn_and_quantise(step - 1)
            if step + X_AHEAD < n_rounds:
                zero_planes(rounds[step + X_AHEAD][0])
            if step == 1:
                small_loads()
            if step == small_step:
                small_transposes()
            if step == small_step + 1:
                small_products()
            if 1 <= step - 2:
                multiply_round(step - 2)

        both = range(ROW_TILES)
        gate = keep.tile([P, ROW_TILES, LSTM_GATES], F32, name="gate")
        base = keep.tile([P, ROW_TILES, 3 * D_H], F32, name="base")
        share = [[keep.tile([P, D_H], F32, name="share%d%d" % (j, rt)) for rt in both] for j in range(3)]
        kept = [keep.tile([P, D_H], F32, name="kept%d" % rt) for rt in both]
        fresh = [keep.tile([P, D_H], F32, name="fresh%d" % rt) for rt in both]
        tanh_c = [keep.tile([P, D_H], F32, name="tanh_c%d" % rt) for rt in both]
        tc_t = [keep.tile([P, D_H], F32, name="tc_t%d" % rt) for rt in both]
        taken = [[keep.tile([P, D_H], F32, name="taken%d%d" % (j, rt)) for rt in both] for j in range(3)]
        rest = [[keep.tile([P, D_H], F32, name="rest%d%d" % (j, rt)) for rt in both] for j in range(3)]
        c_t = keep.tile([P, ROW_TILES, D_H], F32, name="c_t")
        h_t = keep.tile([P, ROW_TILES, D_H], F32, name="h_t")
        s_t = [keep.tile([P, ROW_TILES, D_H], F32, name="s_t%d" % j) for j in range(3)]
        in_gate = [gate[:, rt, 0:D_H] for rt in both]
        forget_gate = [gate[:, rt, D_H : 2 * D_H] for rt in both]
        out_gate = [gate[:, rt, 2 * D_H : 3 * D_H] for rt in both]
        candidate = [gate[:, rt, 3 * D_H : LSTM_GATES] for rt in both]
        m = [row_mask[:, rt : rt + 1] for rt in both]

        def store(result, out):
            nc.sync.dma_start(out=out.rearrange("(rt p) d -> p rt d", p=P), in_=result[:])

        def gates(rt):
            nc.vector.tensor_tensor(out=gate[:, rt, :], in0=acc[0][rt][:], in1=plain[:, rt, 0:LSTM_GATES], op=ALU.add)
            nc.scalar.activation(out=gate[:, rt, 0 : 3 * D_H], in_=gate[:, rt, 0 : 3 * D_H], func=ACT.Sigmoid)
            nc.scalar.activation(out=candidate[rt], in_=candidate[rt], func=ACT.Tanh)

        def cell(rt):
            nc.vector.scalar_tensor_tensor(
                out=kept[rt][:], in0=forget_gate[rt], scalar=m[rt], in1=c_rows[:, rt, :], op0=ALU.mult, op1=ALU.mult
            )
            nc.vector.scalar_tensor_tensor(
                out=fresh[rt][:], in0=in_gate[rt], scalar=m[rt], in1=candidate[rt], op0=ALU.mult, op1=ALU.mult
            )
            nc.vector.tensor_tensor(out=c_t[:, rt, :], in0=kept[rt][:], in1=fresh[rt][:], op=ALU.add)
            nc.scalar.activation(out=tanh_c[rt][:], in_=c_t[:, rt, :], func=ACT.Tanh)

        def hidden(rt):
            nc.vector.tensor_scalar(out=tc_t[rt][:], in0=tanh_c[rt][:], scalar1=m[rt], scalar2=None, op0=ALU.mult)
            nc.vector.scalar_tensor_tensor(
                out=h_t[:, rt, :], in0=tanh_c[rt][:], scalar=m[rt], in1=out_gate[rt], op0=ALU.mult, op1=ALU.mult
            )

        def late_bank(j, rt):
            if j == 0:
                return acc_psum.tile([P, LSTM_GATES], F32, name="late_b0", tag="acc1%d" % rt)
            return turn_psum.tile([P, LSTM_GATES], F32, name="late_b", tag="bank")

        def shared_gate(j, rt):
            nc.vector.tensor_tensor(
                out=share[j][rt][:], in0=late[j][rt][:, 0:D_H], in1=base[:, rt, j * D_H : (j + 1) * D_H], op=ALU.add
            )
            nc.scalar.activation(out=share[j][rt][:], in_=share[j][rt][:], func=ACT.Sigmoid)

        def rest_of(j, rt):
            if j == 0:
                subtracted = out_gate[rt]
            else:
                subtracted = taken[j][rt][:]
            nc.vector.scalar_tensor_tensor(
                out=rest[j][rt][:],
                in0=share[j][rt][:],
                scalar=float(j + 1),
                in1=subtracted,
                op0=ALU.add,
                op1=ALU.subtract,
            )

        def state(j, rt):
            nc.vector.scalar_tensor_tensor(
                out=s_t[j][:, rt, :],
                in0=rest[j][rt][:],
                scalar=1.0 / (j + 1),
                in1=tc_t[rt][:],
                op0=ALU.mult,
                op1=ALU.mult,
            )

        def take_1(rt):
            nc.vector.tensor_tensor(out=taken[1][rt][:], in0=out_gate[rt], in1=s_t[0][:, rt, :], op=ALU.add)

        def take_more(rt):
            nc.vector.tensor_tensor(out=taken[0][rt][:], in0=taken[1][rt][:], in1=s_t[0][:, rt, :], op=ALU.add)

        def take_2(rt):
            nc.vector.tensor_tensor(out=taken[2][rt][:], in0=taken[0][rt][:], in1=s_t[1][:, rt, :], op=ALU.add)

        for rt in both:
            nc.vector.tensor_tensor(
                out=base[:, rt, :], in0=acc[1][rt][:, 0 : 3 * D_H], in1=plain[:, rt, LSTM_GATES:GATES], op=ALU.add
            )
        for rt in both:
            for r in range(late_lstm, n_rounds):
                multiply(acc[0][rt], rt, WINDOWS[0], r, 0, n_rounds - 1)
        late = [[late_bank(j, rt) for rt in both] for j in range(3)]
        for r in range(late_shared, by_gate):
            for i in range(rounds[r][1]):
                for rt in both:
                    for j in range(3):
                        multiply(late[j][rt], rt, WINDOWS[1][j : j + 1], r, late_shared, n_rounds - 1, (i,))
        for j in range(3):
            for r in range(by_gate, n_rounds):
                for i in range(rounds[r][1]):
                    for rt in both:
                        multiply(late[j][rt], rt, WINDOWS[1][j : j + 1], r, late_shared, n_rounds - 1, (i,))

        gates(0)
        cell(0)
        gates(1)
        hidden(0)
        cell(1)
        store(c_t, out_1)
        hidden(1)
        store(h_t, out_0)
        shared_gate(0, 0)
        shared_gate(0, 1)
        rest_of(0, 0)
        rest_of(0, 1)
        state(0, 0)
        state(0, 1)
        store(s_t[0], out_2)
        shared_gate(1, 0)
        take_1(0)
        take_1(1)
        shared_gate(1, 1)
        take_more(0)
        rest_of(1, 0)
        take_more(1)
        rest_of(1, 1)
        state(1, 0)
        state(1, 1)
        store(s_t[1], out_3)
        take_2(0)
        take_2(1)
        shared_gate(2, 0)
        shared_gate(2, 1)
        rest_of(2, 0)
        rest_of(2, 1)
        state(2, 0)
        state(2, 1)
        store(s_t[2], out_4)
